import numpy as np
import ml_dtypes


def mxq(x, axis, fmt="e4m3"):
    dtype, down = {"e4m3": (ml_dtypes.float8_e4m3fn, 7), "e5m2": (ml_dtypes.float8_e5m2, 14)}[fmt]
    v = np.moveaxis(np.asarray(x, np.float32).astype(ml_dtypes.bfloat16).astype(np.float64), axis, -1)
    blocks = v.reshape(v.shape[:-1] + (-1, 32))
    amax = np.abs(blocks).max(-1, keepdims=True)
    byte = np.maximum(np.where(amax > 0, np.frexp(amax)[1] - 1 + 127, 0) - down, 1)
    scale = np.exp2(byte - 127.0)
    codes = (blocks / scale).astype(np.float32).astype(dtype).astype(np.float64)
    return np.moveaxis((codes * scale).reshape(v.shape), -1, axis)


WIDE = False


def mx_kscale(k):
    if not WIDE:
        return np.ones(k)
    levels = np.array([10, -10, 5, -5, 0])
    a = np.random.permutation(np.resize(levels, k // 512 * 4)).reshape(k // 512, 4)
    idx = np.arange(k)
    return np.exp2(a[idx // 512, idx % 128 // 32])


BF16 = ml_dtypes.bfloat16


def bf(x):
    return np.asarray(x, np.float32).astype(BF16)


def f64(x):
    return np.asarray(x).astype(np.float64)


E2M1 = np.array([0.0, 0.5, 1.0, 1.5, 2.0, 3.0, 4.0, 6.0, -0.0, -0.5, -1.0, -1.5, -2.0, -3.0, -4.0, -6.0])


def pack_weight(w, fmt):
    k, n = w.shape
    w = f64(bf(w)).reshape(k // 32, 32, n)
    amax = np.abs(w).max(1)
    if fmt == "e4m3":
        byte = np.frexp(amax)[1] - 1 + 127 - 7
    else:
        mant, ex = np.frexp(amax / 6.0)
        byte = np.where(mant > 0.5, ex, ex - 1) + 127
    byte = np.clip(np.where(amax > 0, byte, 1), 1, 254)
    scaled = (w * np.exp2(127.0 - byte)[:, None, :]).reshape(k, n).astype(np.float32)
    by_word = np.ascontiguousarray(scaled.reshape(k // 512, 128, 4, n).transpose(0, 1, 3, 2))
    if fmt == "e4m3":
        words = by_word.astype(ml_dtypes.float8_e4m3fn).view(np.uint8)
    else:
        c = by_word.astype(ml_dtypes.float4_e2m1fn).view(np.uint8) & 0xF
        words = c[..., 0::2] | (c[..., 1::2] << 4)
    return np.ascontiguousarray(words), np.ascontiguousarray(byte.astype(np.uint8).reshape(k // 512, 16, n))


def unpack_weight(words, scales, fmt):
    g, p, n, _ = words.shape
    if fmt == "e4m3":
        vals = np.ascontiguousarray(words).view(ml_dtypes.float8_e4m3fn).astype(np.float64)
    else:
        nib = np.empty((g, p, n, 4), np.uint8)
        nib[..., 0::2] = words & 0xF
        nib[..., 1::2] = words >> 4
        vals = E2M1[nib]
    vals = vals * np.repeat(np.exp2(scales.astype(np.float64) - 127.0), 8, axis=1)[..., None]
    return vals.transpose(0, 1, 3, 2).reshape(g * 512, n)

def pack4(w):
    words, scales = pack_weight(w, "e2m1")
    return words.reshape(words.shape[0], 128, -1), scales


def unpack4(words, scales):
    return unpack_weight(words.reshape(words.shape[0], 128, -1, 2), scales, "e2m1")


B, S, D, H, DH, F = 1, 256, 1024, 8, 128, 4096
INNER = H * DH
HALF = DH // 2
EPS = 1e-5


def rmsnorm(u, g):
    var = np.mean(np.square(u), axis=-1, keepdims=True)
    return u * (1.0 / np.sqrt(var + EPS)) * g


def rope_interleaved(u, cos, sin):
    u1 = u[..., 0::2]
    u2 = u[..., 1::2]
    c = cos[None, :, None, :]
    s = sin[None, :, None, :]
    o1 = u1 * c - u2 * s
    o2 = u2 * c + u1 * s
    return np.stack([o1, o2], axis=-1).reshape(u.shape)


def setup_inputs():
    s = mx_kscale(D)
    ang = np.random.uniform(0.0, 2.0 * np.pi, (S, HALF))
    hidden_states = bf(np.random.standard_normal((B, S, D)) * s)
    w_q_words, w_q_scales = pack4(np.random.standard_normal((D, INNER)) * 0.02 / np.sqrt(D) / s[:, None])
    w_k_words, w_k_scales = pack4(np.random.standard_normal((D, INNER)) * 0.02 / np.sqrt(D) / s[:, None])
    w_v_words, w_v_scales = pack4(np.random.standard_normal((D, INNER)) * 3.0 / np.sqrt(D) / s[:, None])
    return {"hidden_states": hidden_states,
            "w_q_words": w_q_words,
            "w_q_scales": w_q_scales,
            "w_k_words": w_k_words,
            "w_k_scales": w_k_scales,
            "w_v_words": w_v_words,
            "w_v_scales": w_v_scales,
            "norm_q_w": bf(1.0 + 0.1 * np.random.standard_normal(DH)),
            "norm_k_w": bf(1.0 + 0.1 * np.random.standard_normal(DH)),
            "cos": bf(np.cos(ang)),
            "sin": bf(np.sin(ang))}


def reference(hidden_states, w_q_words, w_q_scales, w_k_words, w_k_scales, w_v_words, w_v_scales, norm_q_w, norm_k_w, cos, sin):
    xq = mxq(f64(hidden_states), 2, "e4m3")
    q = (xq @ unpack4(w_q_words, w_q_scales)).reshape(B, S, H, DH)
    k = (xq @ unpack4(w_k_words, w_k_scales)).reshape(B, S, H, DH)
    v = (xq @ unpack4(w_v_words, w_v_scales)).reshape(B, S, H, DH)
    q = rmsnorm(q, f64(norm_q_w))
    k = rmsnorm(k, f64(norm_k_w))
    q = rope_interleaved(q, f64(cos), f64(sin))
    k = rope_interleaved(k, f64(cos), f64(sin))
    return q, k, v

@@ -1,0 +1,191 @@
+from contextlib import ExitStack
+
+import concourse.mybir as mybir
+from concourse.masks import make_identity
+
+F32 = mybir.dt.float32
+BF16 = mybir.dt.bfloat16
+I32 = mybir.dt.int32
+U32 = mybir.dt.uint32
+U8 = mybir.dt.uint8
+FP8X4 = mybir.dt.float8_e4m3fn_x4
+FP4X4 = mybir.dt.float4_e2m1fn_x4
+ACT = mybir.ActivationFunctionType
+ALU = mybir.AluOpType
+
+P = 128
+PACK = 4
+K_PASS = P * PACK
+TOKENS = 256
+D_MODEL = 1024
+HEADS = 8
+HEAD_DIM = 128
+PAIRS = HEAD_DIM // 2
+EPS = 1e-5
+
+PASSES = D_MODEL // K_PASS
+TOKEN_TILES = TOKENS // P
+BANK_COLS = 512
+BANK_HEADS = BANK_COLS // HEAD_DIM
+BANKS = HEADS * HEAD_DIM // BANK_COLS
+WORDS_PER_PASS = K_PASS // 2
+
+FLOPS = 2 * TOKENS * D_MODEL * 3 * HEADS * HEAD_DIM
+
+
+def load_weight(nc, keep, label, words_in, scales_in):
+    planes = keep.tile([P, PASSES, HEADS * HEAD_DIM], U8, name="planes_" + label, align_bytes=64)
+    nc.vector.memset(planes[:].bitcast(I32), 0)
+    by_row = scales_in.rearrange("g (quad r) n -> r quad g n", r=4)
+    for r in range(4):
+        nc.sync.dma_start(out=planes[r:P:32, :, :].bitcast(I32), in_=by_row[r].bitcast(I32))
+    words = keep.tile([P, PASSES, 2 * HEADS * HEAD_DIM], U8, name="words_" + label, align_bytes=64)
+    nc.sync.dma_start(out=words[:].bitcast(I32), in_=words_in.rearrange("g p b -> p g b").bitcast(I32))
+    return words, planes
+
+
+def quantise_tokens(nc, keep, psum_x, copy_out, m, x_sb, identity):
+    x_words = x_sb[:].bitcast(F32)
+    flipped = psum_x.tile([P, PASSES, 2, P], F32, name="flipped")
+    for g in range(PASSES):
+        for u in range(2):
+            first = WORDS_PER_PASS * g + u
+            nc.tensor.transpose(flipped[:, g, u, :], x_words[:, first : WORDS_PER_PASS * (g + 1) : 2], identity[:])
+    grouped = keep.tile([P, PASSES, P, PACK], BF16, name="grouped%d" % m, align_bytes=64)
+    copy_out(out=grouped[:].bitcast(F32), in_=flipped[:].rearrange("p g u r -> p g r u"))
+    codes = keep.tile([P, PASSES, P], U32, name="x_codes%d" % m, align_bytes=64)
+    scales = keep.tile([P, PASSES, P], U8, name="x_scales%d" % m, align_bytes=64)
+    nc.vector.quantize_mx(
+        out=codes[:].rearrange("p g r -> p (g r)").bitcast(FP8X4),
+        scales=scales[:].rearrange("p g r -> p (g r)"),
+        in_=grouped[:].rearrange("p g r t -> p (g r t)"),
+    )
+    return codes, scales
+
+
+def project(nc, psum_acc, x_codes, x_scales, words, planes, bank):
+    acc = psum_acc.tile([P, BANK_COLS], F32, name="acc")
+    for g in range(PASSES):
+        nc.tensor.matmul_mx(
+            out=acc[:],
+            lhsT=x_codes[:, g, :].bitcast(FP8X4),
+            lhsT_scale=x_scales[:, g, :],
+            rhs=words[:, g, 2 * BANK_COLS * bank : 2 * BANK_COLS * (bank + 1)].bitcast(FP4X4),
+            rhs_scale=planes[:, g, BANK_COLS * bank : BANK_COLS * (bank + 1)],
+            start=(g == 0),
+            stop=(g == PASSES - 1),
+        )
+    return acc
+
+
+def norm_and_rotate(nc, work, acc, table):
+    squares = work.tile([P, BANK_COLS], BF16, name="squares")
+    sum_sq = work.tile([P, BANK_HEADS], F32, name="sum_sq")
+    for h in range(BANK_HEADS):
+        cols = slice(HEAD_DIM * h, HEAD_DIM * (h + 1))
+        nc.scalar.activation(out=squares[:, cols], in_=acc[:, cols], func=ACT.Square, accum_out=sum_sq[:, h : h + 1])
+    rms = work.tile([P, BANK_HEADS], F32, name="rms")
+    nc.scalar.activation(out=rms[:], in_=sum_sq[:], func=ACT.Sqrt, scale=1.0 / HEAD_DIM, bias=EPS)
+    inv_rms = work.tile([P, BANK_HEADS], F32, name="inv_rms")
+    nc.vector.reciprocal(out=inv_rms[:], in_=rms[:])
+
+    shape = [P, 2, 2, BANK_HEADS, PAIRS]
+    products = work.tile(shape, F32, name="products")
+    nc.vector.tensor_tensor(
+        out=products[:],
+        in0=acc[:].rearrange("p (h i a) -> p a h i", h=BANK_HEADS, a=2).unsqueeze(2).to_broadcast(shape),
+        in1=table.unsqueeze(3).to_broadcast(shape),
+        op=ALU.mult,
+    )
+    rotated = work.tile([P, BANK_HEADS, HEAD_DIM], F32, name="rotated")
+    nc.vector.tensor_tensor(
+        out=rotated[:].rearrange("p h (i b) -> p h i b", b=2),
+        in0=products[:, 0].rearrange("p b h i -> p h i b"),
+        in1=products[:, 1].rearrange("p b h i -> p h i b"),
+        op=ALU.add,
+    )
+    finished = work.tile([P, BANK_HEADS, HEAD_DIM], F32, name="finished")
+    for h in range(BANK_HEADS):
+        nc.scalar.activation(out=finished[:, h, :], in_=rotated[:, h, :], func=ACT.Copy, scale=inv_rms[:, h : h + 1])
+    return finished
+
+
+def tile_flux2parallelselfattention_pa_kernel(
+    tc,
+    hidden_states,
+    w_q_words,
+    w_q_scales,
+    w_k_words,
+    w_k_scales,
+    w_v_words,
+    w_v_scales,
+    norm_q_w,
+    norm_k_w,
+    cos,
+    sin,
+    out_0,
+    out_1,
+    out_2,
+):
+    nc = tc.nc
+    with ExitStack() as ctx:
+        keep = ctx.enter_context(tc.tile_pool(name="keep", bufs=1))
+        work = ctx.enter_context(tc.tile_pool(name="work", bufs=3))
+        psum_x = ctx.enter_context(tc.psum_pool(name="psum_x", bufs=2))
+        psum_acc = ctx.enter_context(tc.psum_pool(name="psum_acc", bufs=6))
+
+        one = keep.tile([P, 1], F32, name="one")
+        nc.vector.memset(one[:], 1.0)
+        warm = keep.tile([P, 1], F32, name="warm")
+        nc.scalar.activation(out=warm[:], in_=one[:], func=ACT.Sqrt)
+
+        trig = keep.tile([P, TOKEN_TILES, 2, PAIRS], BF16, name="trig")
+        nc.gpsimd.dma_start(out=trig[:, :, 0, :], in_=cos.rearrange("(m p) i -> p m i", p=P))
+        nc.gpsimd.dma_start(out=trig[:, :, 1, :], in_=sin.rearrange("(m p) i -> p m i", p=P))
+        gains = keep.tile([P, 2, HEAD_DIM], BF16, name="gains")
+        nc.gpsimd.dma_start(out=gains[:, 0, :], in_=norm_q_w.partition_broadcast(P))
+        nc.gpsimd.dma_start(out=gains[:, 1, :], in_=norm_k_w.partition_broadcast(P))
+
+        x_rows = hidden_states.rearrange("b (m p) d -> m p (b d)", p=P)
+        x_tiles = []
+        for m in range(TOKEN_TILES):
+            x_sb = keep.tile([P, D_MODEL], BF16, name="x_sb%d" % m)
+            nc.sync.dma_start(out=x_sb[:], in_=x_rows[m])
+            x_tiles.append(x_sb)
+        weights = [
+            load_weight(nc, keep, "q", w_q_words, w_q_scales),
+            load_weight(nc, keep, "k", w_k_words, w_k_scales),
+            load_weight(nc, keep, "v", w_v_words, w_v_scales),
+        ]
+
+        identity = keep.tile([P, P], F32, name="identity")
+        make_identity(nc, identity[:])
+        x_mx = [
+            quantise_tokens(nc, keep, psum_x, nc.vector.tensor_copy, 0, x_tiles[0], identity),
+            quantise_tokens(nc, keep, psum_x, nc.scalar.copy, 1, x_tiles[1], identity),
+        ]
+
+        rotation = keep.tile([P, TOKEN_TILES, 2, 2, PAIRS], F32, name="rotation")
+        nc.vector.tensor_copy(out=rotation[:, :, 0, :, :], in_=trig[:])
+        nc.vector.tensor_scalar_mul(out=rotation[:, :, 1, 0, :], in0=trig[:, :, 1, :], scalar1=-1.0)
+        nc.vector.tensor_copy(out=rotation[:, :, 1, 1, :], in_=trig[:, :, 0, :])
+        tables = keep.tile([P, TOKEN_TILES, 2, 2, 2, PAIRS], F32, name="tables")
+        for m in range(TOKEN_TILES):
+            for w in range(2):
+                gain = gains[:, w, :].rearrange("p (i a) -> p a i", a=2).unsqueeze(2).to_broadcast([P, 2, 2, PAIRS])
+                nc.vector.tensor_tensor(out=tables[:, m, w], in0=rotation[:, m], in1=gain, op=ALU.mult)
+
+        outs = [o.rearrange("b (m p) h d -> m p (b h) d", p=P) for o in (out_0, out_1, out_2)]
+        for m in range(TOKEN_TILES):
+            x_codes, x_scales = x_mx[m]
+            for w in range(3):
+                words, planes = weights[w]
+                for bank in range(BANKS):
+                    acc = project(nc, psum_acc, x_codes, x_scales, words, planes, bank)
+                    if w < 2:
+                        finished = norm_and_rotate(nc, work, acc, tables[:, m, w])
+                    else:
+                        finished = work.tile([P, BANK_HEADS, HEAD_DIM], F32, name="finished")
+                        nc.scalar.copy(out=finished[:].rearrange("p h d -> p (h d)"), in_=acc[:])
+                    heads = slice(BANK_HEADS * bank, BANK_HEADS * (bank + 1))
+                    nc.sync.dma_start(out=outs[w][m][:, heads, :], in_=finished[:])

@@ -44,9 +44,9 @@ def load_weight(nc, keep, label, words_in, scales_in):
     return words, planes
 
 
-def quantise_tokens(nc, keep, psum_x, copy_out, m, x_sb, identity):
+def quantise_tokens(nc, keep, psum, copy_out, m, x_sb, identity):
     x_words = x_sb[:].bitcast(F32)
-    flipped = psum_x.tile([P, PASSES, 2, P], F32, name="flipped")
+    flipped = psum.tile([P, PASSES, 2, P], F32, name="flipped", tag="bank")
     for g in range(PASSES):
         for u in range(2):
             first = WORDS_PER_PASS * g + u
@@ -63,8 +63,8 @@ def quantise_tokens(nc, keep, psum_x, copy_out, m, x_sb, identity):
     return codes, scales
 
 
-def project(nc, psum_acc, x_codes, x_scales, words, planes, bank):
-    acc = psum_acc.tile([P, BANK_COLS], F32, name="acc")
+def project(nc, psum, x_codes, x_scales, words, planes, bank):
+    acc = psum.tile([P, BANK_COLS], F32, name="acc", tag="bank")
     for g in range(PASSES):
         nc.tensor.matmul_mx(
             out=acc[:],
@@ -78,17 +78,7 @@ def project(nc, psum_acc, x_codes, x_scales, words, planes, bank):
     return acc
 
 
-def norm_and_rotate(nc, work, acc, table):
-    squares = work.tile([P, BANK_COLS], BF16, name="squares")
-    sum_sq = work.tile([P, BANK_HEADS], F32, name="sum_sq")
-    for h in range(BANK_HEADS):
-        cols = slice(HEAD_DIM * h, HEAD_DIM * (h + 1))
-        nc.scalar.activation(out=squares[:, cols], in_=acc[:, cols], func=ACT.Square, accum_out=sum_sq[:, h : h + 1])
-    rms = work.tile([P, BANK_HEADS], F32, name="rms")
-    nc.scalar.activation(out=rms[:], in_=sum_sq[:], func=ACT.Sqrt, scale=1.0 / HEAD_DIM, bias=EPS)
-    inv_rms = work.tile([P, BANK_HEADS], F32, name="inv_rms")
-    nc.vector.reciprocal(out=inv_rms[:], in_=rms[:])
-
+def rotate(nc, work, acc, table):
     shape = [P, 2, 2, BANK_HEADS, PAIRS]
     products = work.tile(shape, F32, name="products")
     nc.vector.tensor_tensor(
@@ -97,17 +87,32 @@ def norm_and_rotate(nc, work, acc, table):
         in1=table.unsqueeze(3).to_broadcast(shape),
         op=ALU.mult,
     )
-    rotated = work.tile([P, BANK_HEADS, HEAD_DIM], F32, name="rotated")
-    nc.vector.tensor_tensor(
-        out=rotated[:].rearrange("p h (i b) -> p h i b", b=2),
-        in0=products[:, 0].rearrange("p b h i -> p h i b"),
-        in1=products[:, 1].rearrange("p b h i -> p h i b"),
-        op=ALU.add,
-    )
+    rotated = work.tile([P, 2, BANK_HEADS, PAIRS], F32, name="rotated")
+    nc.gpsimd.tensor_tensor(out=rotated[:], in0=products[:, 0], in1=products[:, 1], op=ALU.add)
+    return rotated
+
+
+def inverse_rms(nc, work, acc):
+    squares = work.tile([P, BANK_COLS], BF16, name="squares")
+    sum_sq = work.tile([P, BANK_HEADS], F32, name="sum_sq")
+    for h in range(BANK_HEADS):
+        cols = slice(HEAD_DIM * h, HEAD_DIM * (h + 1))
+        nc.scalar.activation(out=squares[:, cols], in_=acc[:, cols], func=ACT.Square, accum_out=sum_sq[:, h : h + 1])
+    inv_rms = work.tile([P, BANK_HEADS], F32, name="inv_rms")
+    nc.scalar.activation(out=inv_rms[:], in_=sum_sq[:], func=ACT.Abs_reciprocal_sqrt, scale=1.0 / HEAD_DIM, bias=EPS)
+    return inv_rms
+
+
+def finish(nc, work, rotated, inv_rms, out_rows):
     finished = work.tile([P, BANK_HEADS, HEAD_DIM], F32, name="finished")
     for h in range(BANK_HEADS):
-        nc.scalar.activation(out=finished[:, h, :], in_=rotated[:, h, :], func=ACT.Copy, scale=inv_rms[:, h : h + 1])
-    return finished
+        nc.scalar.activation(
+            out=finished[:, h, :].rearrange("p (i b) -> p i b", b=2),
+            in_=rotated[:, :, h, :].rearrange("p b i -> p i b"),
+            func=ACT.Copy,
+            scale=inv_rms[:, h : h + 1],
+        )
+    nc.sync.dma_start(out=out_rows, in_=finished[:])
 
 
 def tile_flux2parallelselfattention_pa_kernel(
@@ -130,62 +135,62 @@ def tile_flux2parallelselfattention_pa_kernel(
     nc = tc.nc
     with ExitStack() as ctx:
         keep = ctx.enter_context(tc.tile_pool(name="keep", bufs=1))
-        work = ctx.enter_context(tc.tile_pool(name="work", bufs=3))
-        psum_x = ctx.enter_context(tc.psum_pool(name="psum_x", bufs=2))
-        psum_acc = ctx.enter_context(tc.psum_pool(name="psum_acc", bufs=6))
+        work = ctx.enter_context(tc.tile_pool(name="work", bufs=3 * TOKEN_TILES * BANKS))
+        psum = ctx.enter_context(tc.psum_pool(name="psum", bufs=8))
+
+        gains = keep.tile([P, 2, HEAD_DIM], BF16, name="gains")
+        nc.gpsimd.dma_start(out=gains[:, 0, :], in_=norm_q_w.partition_broadcast(P))
+        nc.gpsimd.dma_start(out=gains[:, 1, :], in_=norm_k_w.partition_broadcast(P))
+        trig = keep.tile([P, TOKEN_TILES, 2, PAIRS], BF16, name="trig")
+        nc.scalar.dma_start(out=trig[:, :, 0, :], in_=cos.rearrange("(m p) i -> p m i", p=P))
+        nc.scalar.dma_start(out=trig[:, :, 1, :], in_=sin.rearrange("(m p) i -> p m i", p=P))
+        x_rows = hidden_states.rearrange("b (m p) d -> m p (b d)", p=P)
+        x_tiles = [keep.tile([P, D_MODEL], BF16, name="x_sb%d" % m) for m in range(TOKEN_TILES)]
+        nc.sync.dma_start(out=x_tiles[0][:], in_=x_rows[0])
+        weight_q = load_weight(nc, keep, "q", w_q_words, w_q_scales)
+        nc.sync.dma_start(out=x_tiles[1][:], in_=x_rows[1])
+        weight_k = load_weight(nc, keep, "k", w_k_words, w_k_scales)
+        weight_v = load_weight(nc, keep, "v", w_v_words, w_v_scales)
+
+        identity = keep.tile([P, P], F32, name="identity")
+        make_identity(nc, identity[:])
 
         one = keep.tile([P, 1], F32, name="one")
         nc.vector.memset(one[:], 1.0)
         warm = keep.tile([P, 1], F32, name="warm")
-        nc.scalar.activation(out=warm[:], in_=one[:], func=ACT.Sqrt)
-
-        trig = keep.tile([P, TOKEN_TILES, 2, PAIRS], BF16, name="trig")
-        nc.gpsimd.dma_start(out=trig[:, :, 0, :], in_=cos.rearrange("(m p) i -> p m i", p=P))
-        nc.gpsimd.dma_start(out=trig[:, :, 1, :], in_=sin.rearrange("(m p) i -> p m i", p=P))
-        gains = keep.tile([P, 2, HEAD_DIM], BF16, name="gains")
-        nc.gpsimd.dma_start(out=gains[:, 0, :], in_=norm_q_w.partition_broadcast(P))
-        nc.gpsimd.dma_start(out=gains[:, 1, :], in_=norm_k_w.partition_broadcast(P))
-
-        x_rows = hidden_states.rearrange("b (m p) d -> m p (b d)", p=P)
-        x_tiles = []
-        for m in range(TOKEN_TILES):
-            x_sb = keep.tile([P, D_MODEL], BF16, name="x_sb%d" % m)
-            nc.sync.dma_start(out=x_sb[:], in_=x_rows[m])
-            x_tiles.append(x_sb)
-        weights = [
-            load_weight(nc, keep, "q", w_q_words, w_q_scales),
-            load_weight(nc, keep, "k", w_k_words, w_k_scales),
-            load_weight(nc, keep, "v", w_v_words, w_v_scales),
-        ]
-
-        identity = keep.tile([P, P], F32, name="identity")
-        make_identity(nc, identity[:])
-        x_mx = [
-            quantise_tokens(nc, keep, psum_x, nc.vector.tensor_copy, 0, x_tiles[0], identity),
-            quantise_tokens(nc, keep, psum_x, nc.scalar.copy, 1, x_tiles[1], identity),
-        ]
+        nc.scalar.activation(out=warm[:], in_=one[:], func=ACT.Abs_reciprocal_sqrt)
 
         rotation = keep.tile([P, TOKEN_TILES, 2, 2, PAIRS], F32, name="rotation")
-        nc.vector.tensor_copy(out=rotation[:, :, 0, :, :], in_=trig[:])
-        nc.vector.tensor_scalar_mul(out=rotation[:, :, 1, 0, :], in0=trig[:, :, 1, :], scalar1=-1.0)
-        nc.vector.tensor_copy(out=rotation[:, :, 1, 1, :], in_=trig[:, :, 0, :])
+        nc.scalar.copy(out=rotation[:, :, 0, :, :], in_=trig[:])
+        nc.scalar.mul(out=rotation[:, :, 1, 0, :], in_=trig[:, :, 1, :], mul=-1.0)
+        nc.scalar.copy(out=rotation[:, :, 1, 1, :], in_=trig[:, :, 0, :])
         tables = keep.tile([P, TOKEN_TILES, 2, 2, 2, PAIRS], F32, name="tables")
         for m in range(TOKEN_TILES):
             for w in range(2):
                 gain = gains[:, w, :].rearrange("p (i a) -> p a i", a=2).unsqueeze(2).to_broadcast([P, 2, 2, PAIRS])
                 nc.vector.tensor_tensor(out=tables[:, m, w], in0=rotation[:, m], in1=gain, op=ALU.mult)
 
+        x_mx = [quantise_tokens(nc, keep, psum, nc.scalar.copy, m, x_tiles[m], identity) for m in range(TOKEN_TILES)]
+
         outs = [o.rearrange("b (m p) h d -> m p (b h) d", p=P) for o in (out_0, out_1, out_2)]
+        heads = [slice(BANK_HEADS * bank, BANK_HEADS * (bank + 1)) for bank in range(BANKS)]
+
         for m in range(TOKEN_TILES):
             x_codes, x_scales = x_mx[m]
-            for w in range(3):
-                words, planes = weights[w]
-                for bank in range(BANKS):
-                    acc = project(nc, psum_acc, x_codes, x_scales, words, planes, bank)
-                    if w < 2:
-                        finished = norm_and_rotate(nc, work, acc, tables[:, m, w])
-                    else:
-                        finished = work.tile([P, BANK_HEADS, HEAD_DIM], F32, name="finished")
-                        nc.scalar.copy(out=finished[:].rearrange("p h d -> p (h d)"), in_=acc[:])
-                    heads = slice(BANK_HEADS * bank, BANK_HEADS * (bank + 1))
-                    nc.sync.dma_start(out=outs[w][m][:, heads, :], in_=finished[:])
+            for w, (words, planes) in enumerate((weight_q, weight_k)):
+                acc = [project(nc, psum, x_codes, x_scales, words, planes, bank) for bank in range(BANKS)]
+                rotated_0 = rotate(nc, work, acc[0], tables[:, m, w])
+                inv_rms_1 = inverse_rms(nc, work, acc[1])
+                inv_rms_0 = inverse_rms(nc, work, acc[0])
+                rotated_1 = rotate(nc, work, acc[1], tables[:, m, w])
+                finish(nc, work, rotated_0, inv_rms_0, outs[w][m][:, heads[0], :])
+                finish(nc, work, rotated_1, inv_rms_1, outs[w][m][:, heads[1], :])
+
+        words, planes = weight_v
+        for m in range(TOKEN_TILES):
+            x_codes, x_scales = x_mx[m]
+            for bank in range(BANKS):
+                acc_v = project(nc, psum, x_codes, x_scales, words, planes, bank)
+                values = work.tile([P, BANK_HEADS, HEAD_DIM], F32, name="values")
+                nc.vector.tensor_copy(out=values[:].rearrange("p h d -> p (h d)"), in_=acc_v[:])
+                nc.sync.dma_start(out=outs[2][m][:, heads[bank], :], in_=values[:])

@@ -138,9 +138,10 @@ def tile_flux2parallelselfattention_pa_kernel(
         work = ctx.enter_context(tc.tile_pool(name="work", bufs=3 * TOKEN_TILES * BANKS))
         psum = ctx.enter_context(tc.psum_pool(name="psum", bufs=8))
 
-        gains = keep.tile([P, 2, HEAD_DIM], BF16, name="gains")
-        nc.gpsimd.dma_start(out=gains[:, 0, :], in_=norm_q_w.partition_broadcast(P))
-        nc.gpsimd.dma_start(out=gains[:, 1, :], in_=norm_k_w.partition_broadcast(P))
+        gain_rows = keep.tile([P, 2, HEAD_DIM], BF16, name="gain_rows")
+        nc.vector.memset(gain_rows[:], 0.0)
+        nc.gpsimd.dma_start(out=gain_rows[0:1, 0, :], in_=norm_q_w.unsqueeze(0))
+        nc.gpsimd.dma_start(out=gain_rows[0:1, 1, :], in_=norm_k_w.unsqueeze(0))
         trig = keep.tile([P, TOKEN_TILES, 2, PAIRS], BF16, name="trig")
         nc.scalar.dma_start(out=trig[:, :, 0, :], in_=cos.rearrange("(m p) i -> p m i", p=P))
         nc.scalar.dma_start(out=trig[:, :, 1, :], in_=sin.rearrange("(m p) i -> p m i", p=P))
@@ -164,6 +165,10 @@ def tile_flux2parallelselfattention_pa_kernel(
         nc.scalar.copy(out=rotation[:, :, 0, :, :], in_=trig[:])
         nc.scalar.mul(out=rotation[:, :, 1, 0, :], in_=trig[:, :, 1, :], mul=-1.0)
         nc.scalar.copy(out=rotation[:, :, 1, 1, :], in_=trig[:, :, 0, :])
+        ones = keep.tile([P, P], BF16, name="ones")
+        nc.vector.memset(ones[:], 1.0)
+        gains = psum.tile([P, 2, HEAD_DIM], F32, name="gains", tag="bank")
+        nc.tensor.matmul(out=gains[:], lhsT=ones[:], rhs=gain_rows[:], start=True, stop=True)
         tables = keep.tile([P, TOKEN_TILES, 2, 2, 2, PAIRS], F32, name="tables")
         for m in range(TOKEN_TILES):
             for w in range(2):

@@ -78,20 +78,6 @@ def project(nc, psum, x_codes, x_scales, words, planes, bank):
     return acc
 
 
-def rotate(nc, work, acc, table):
-    shape = [P, 2, 2, BANK_HEADS, PAIRS]
-    products = work.tile(shape, F32, name="products")
-    nc.vector.tensor_tensor(
-        out=products[:],
-        in0=acc[:].rearrange("p (h i a) -> p a h i", h=BANK_HEADS, a=2).unsqueeze(2).to_broadcast(shape),
-        in1=table.unsqueeze(3).to_broadcast(shape),
-        op=ALU.mult,
-    )
-    rotated = work.tile([P, 2, BANK_HEADS, PAIRS], F32, name="rotated")
-    nc.gpsimd.tensor_tensor(out=rotated[:], in0=products[:, 0], in1=products[:, 1], op=ALU.add)
-    return rotated
-
-
 def inverse_rms(nc, work, acc):
     squares = work.tile([P, BANK_COLS], BF16, name="squares")
     sum_sq = work.tile([P, BANK_HEADS], F32, name="sum_sq")
@@ -103,15 +89,22 @@ def inverse_rms(nc, work, acc):
     return inv_rms
 
 
-def finish(nc, work, rotated, inv_rms, out_rows):
-    finished = work.tile([P, BANK_HEADS, HEAD_DIM], F32, name="finished")
+def norm_and_rotate(nc, work, acc, inv_rms, table, out_rows):
+    products = work.tile([P, BANK_HEADS, HEAD_DIM, 2], F32, name="products")
     for h in range(BANK_HEADS):
-        nc.scalar.activation(
-            out=finished[:, h, :].rearrange("p (i b) -> p i b", b=2),
-            in_=rotated[:, :, h, :].rearrange("p b i -> p i b"),
-            func=ACT.Copy,
-            scale=inv_rms[:, h : h + 1],
+        nc.vector.scalar_tensor_tensor(
+            out=products[:, h],
+            in0=acc[:, HEAD_DIM * h : HEAD_DIM * (h + 1)].unsqueeze(2).to_broadcast([P, HEAD_DIM, 2]),
+            scalar=inv_rms[:, h : h + 1],
+            in1=table,
+            op0=ALU.mult,
+            op1=ALU.mult,
         )
+    by_feature = products[:].rearrange("p h (i a) b -> p a (h i) b", a=2)
+    finished = work.tile([P, BANK_HEADS, HEAD_DIM], F32, name="finished")
+    nc.gpsimd.tensor_tensor(
+        out=finished[:].rearrange("p h (i b) -> p (h i) b", b=2), in0=by_feature[:, 0], in1=by_feature[:, 1], op=ALU.add
+    )
     nc.sync.dma_start(out=out_rows, in_=finished[:])
 
 
@@ -161,6 +154,8 @@ def tile_flux2parallelselfattention_pa_kernel(
         warm = keep.tile([P, 1], F32, name="warm")
         nc.scalar.activation(out=warm[:], in_=one[:], func=ACT.Abs_reciprocal_sqrt)
 
+        x_mx = [quantise_tokens(nc, keep, psum, nc.scalar.copy, m, x_tiles[m], identity) for m in range(TOKEN_TILES)]
+
         rotation = keep.tile([P, TOKEN_TILES, 2, 2, PAIRS], F32, name="rotation")
         nc.scalar.copy(out=rotation[:, :, 0, :, :], in_=trig[:])
         nc.scalar.mul(out=rotation[:, :, 1, 0, :], in_=trig[:, :, 1, :], mul=-1.0)
@@ -169,13 +164,15 @@ def tile_flux2parallelselfattention_pa_kernel(
         nc.vector.memset(ones[:], 1.0)
         gains = psum.tile([P, 2, HEAD_DIM], F32, name="gains", tag="bank")
         nc.tensor.matmul(out=gains[:], lhsT=ones[:], rhs=gain_rows[:], start=True, stop=True)
-        tables = keep.tile([P, TOKEN_TILES, 2, 2, 2, PAIRS], F32, name="tables")
+        tables = keep.tile([P, TOKEN_TILES, 2, HEAD_DIM, 2], F32, name="tables")
         for m in range(TOKEN_TILES):
             for w in range(2):
-                gain = gains[:, w, :].rearrange("p (i a) -> p a i", a=2).unsqueeze(2).to_broadcast([P, 2, 2, PAIRS])
-                nc.vector.tensor_tensor(out=tables[:, m, w], in0=rotation[:, m], in1=gain, op=ALU.mult)
-
-        x_mx = [quantise_tokens(nc, keep, psum, nc.scalar.copy, m, x_tiles[m], identity) for m in range(TOKEN_TILES)]
+                nc.vector.tensor_tensor(
+                    out=tables[:, m, w].rearrange("p (i a) b -> p i a b", a=2),
+                    in0=rotation[:, m].rearrange("p a b i -> p i a b"),
+                    in1=gains[:, w, :].rearrange("p (i a) -> p i a", a=2).unsqueeze(3).to_broadcast([P, PAIRS, 2, 2]),
+                    op=ALU.mult,
+                )
 
         outs = [o.rearrange("b (m p) h d -> m p (b h) d", p=P) for o in (out_0, out_1, out_2)]
         heads = [slice(BANK_HEADS * bank, BANK_HEADS * (bank + 1)) for bank in range(BANKS)]
@@ -183,13 +180,10 @@ def tile_flux2parallelselfattention_pa_kernel(
         for m in range(TOKEN_TILES):
             x_codes, x_scales = x_mx[m]
             for w, (words, planes) in enumerate((weight_q, weight_k)):
-                acc = [project(nc, psum, x_codes, x_scales, words, planes, bank) for bank in range(BANKS)]
-                rotated_0 = rotate(nc, work, acc[0], tables[:, m, w])
-                inv_rms_1 = inverse_rms(nc, work, acc[1])
-                inv_rms_0 = inverse_rms(nc, work, acc[0])
-                rotated_1 = rotate(nc, work, acc[1], tables[:, m, w])
-                finish(nc, work, rotated_0, inv_rms_0, outs[w][m][:, heads[0], :])
-                finish(nc, work, rotated_1, inv_rms_1, outs[w][m][:, heads[1], :])
+                for bank in range(BANKS):
+                    acc = project(nc, psum, x_codes, x_scales, words, planes, bank)
+                    inv_rms = inverse_rms(nc, work, acc)
+                    norm_and_rotate(nc, work, acc, inv_rms, tables[:, m, w], outs[w][m][:, heads[bank], :])
 
         words, planes = weight_v
         for m in range(TOKEN_TILES):
@@ -197,5 +191,5 @@ def tile_flux2parallelselfattention_pa_kernel(
             for bank in range(BANKS):
                 acc_v = project(nc, psum, x_codes, x_scales, words, planes, bank)
                 values = work.tile([P, BANK_HEADS, HEAD_DIM], F32, name="values")
-                nc.vector.tensor_copy(out=values[:].rearrange("p h d -> p (h d)"), in_=acc_v[:])
+                nc.scalar.copy(out=values[:].rearrange("p h d -> p (h d)"), in_=acc_v[:])
                 nc.sync.dma_start(out=outs[2][m][:, heads[bank], :], in_=values[:])

@@ -34,42 +34,43 @@ FLOPS = 2 * TOKENS * D_MODEL * 3 * HEADS * HEAD_DIM
 
 
 def load_weight(nc, keep, label, words_in, scales_in):
+    words = keep.tile([P, PASSES, 2 * HEADS * HEAD_DIM], U8, name="words_" + label, align_bytes=64)
+    nc.sync.dma_start(out=words[:].bitcast(I32), in_=words_in.rearrange("g p b -> p g b").bitcast(I32))
     planes = keep.tile([P, PASSES, HEADS * HEAD_DIM], U8, name="planes_" + label, align_bytes=64)
     nc.vector.memset(planes[:].bitcast(I32), 0)
     by_row = scales_in.rearrange("g (quad r) n -> r quad g n", r=4)
     for r in range(4):
         nc.sync.dma_start(out=planes[r:P:32, :, :].bitcast(I32), in_=by_row[r].bitcast(I32))
-    words = keep.tile([P, PASSES, 2 * HEADS * HEAD_DIM], U8, name="words_" + label, align_bytes=64)
-    nc.sync.dma_start(out=words[:].bitcast(I32), in_=words_in.rearrange("g p b -> p g b").bitcast(I32))
     return words, planes
 
 
-def quantise_tokens(nc, keep, psum, copy_out, m, x_sb, identity):
+def quantise_tokens(nc, keep, psum, m, x_sb, identity):
     x_words = x_sb[:].bitcast(F32)
-    flipped = psum.tile([P, PASSES, 2, P], F32, name="flipped", tag="bank")
+    quantised = []
     for g in range(PASSES):
+        flipped = psum.tile([P, 2, P], F32, name="flipped", tag="bank")
         for u in range(2):
             first = WORDS_PER_PASS * g + u
-            nc.tensor.transpose(flipped[:, g, u, :], x_words[:, first : WORDS_PER_PASS * (g + 1) : 2], identity[:])
-    grouped = keep.tile([P, PASSES, P, PACK], BF16, name="grouped%d" % m, align_bytes=64)
-    copy_out(out=grouped[:].bitcast(F32), in_=flipped[:].rearrange("p g u r -> p g r u"))
-    codes = keep.tile([P, PASSES, P], U32, name="x_codes%d" % m, align_bytes=64)
-    scales = keep.tile([P, PASSES, P], U8, name="x_scales%d" % m, align_bytes=64)
-    nc.vector.quantize_mx(
-        out=codes[:].rearrange("p g r -> p (g r)").bitcast(FP8X4),
-        scales=scales[:].rearrange("p g r -> p (g r)"),
-        in_=grouped[:].rearrange("p g r t -> p (g r t)"),
-    )
-    return codes, scales
+            nc.tensor.transpose(flipped[:, u, :], x_words[:, first : WORDS_PER_PASS * (g + 1) : 2], identity[:])
+        grouped = keep.tile([P, P, PACK], BF16, name="grouped%d%d" % (m, g), align_bytes=64)
+        nc.scalar.copy(out=grouped[:].bitcast(F32), in_=flipped[:].rearrange("p u r -> p r u"))
+        codes = keep.tile([P, P], U32, name="x_codes%d%d" % (m, g), align_bytes=64)
+        scales = keep.tile([P, P], U8, name="x_scales%d%d" % (m, g), align_bytes=64)
+        nc.vector.quantize_mx(
+            out=codes[:].bitcast(FP8X4), scales=scales[:], in_=grouped[:].rearrange("p r t -> p (r t)")
+        )
+        quantised.append((codes, scales))
+    return quantised
 
 
-def project(nc, psum, x_codes, x_scales, words, planes, bank):
+def project(nc, psum, x_mx, words, planes, bank):
     acc = psum.tile([P, BANK_COLS], F32, name="acc", tag="bank")
     for g in range(PASSES):
+        x_codes, x_scales = x_mx[g]
         nc.tensor.matmul_mx(
             out=acc[:],
-            lhsT=x_codes[:, g, :].bitcast(FP8X4),
-            lhsT_scale=x_scales[:, g, :],
+            lhsT=x_codes[:].bitcast(FP8X4),
+            lhsT_scale=x_scales[:],
             rhs=words[:, g, 2 * BANK_COLS * bank : 2 * BANK_COLS * (bank + 1)].bitcast(FP4X4),
             rhs_scale=planes[:, g, BANK_COLS * bank : BANK_COLS * (bank + 1)],
             start=(g == 0),
@@ -89,7 +90,7 @@ def inverse_rms(nc, work, acc):
     return inv_rms
 
 
-def norm_and_rotate(nc, work, acc, inv_rms, table, out_rows):
+def norm_and_rotate(nc, work, adder, acc, inv_rms, table, out_rows):
     products = work.tile([P, BANK_HEADS, HEAD_DIM, 2], F32, name="products")
     for h in range(BANK_HEADS):
         nc.vector.scalar_tensor_tensor(
@@ -102,10 +103,28 @@ def norm_and_rotate(nc, work, acc, inv_rms, table, out_rows):
         )
     by_feature = products[:].rearrange("p h (i a) b -> p a (h i) b", a=2)
     finished = work.tile([P, BANK_HEADS, HEAD_DIM], F32, name="finished")
-    nc.gpsimd.tensor_tensor(
+    adder.tensor_tensor(
         out=finished[:].rearrange("p h (i b) -> p (h i) b", b=2), in0=by_feature[:, 0], in1=by_feature[:, 1], op=ALU.add
     )
     nc.sync.dma_start(out=out_rows, in_=finished[:])
+
+
+def rotary_tables(nc, keep, m, trig, gains):
+    rotation = keep.tile([P, 2, 2, PAIRS], F32, name="rotation%d" % m)
+    nc.scalar.copy(out=rotation[:, 0, :, :], in_=trig[:, m, :, :])
+    nc.scalar.mul(out=rotation[:, 1, 0, :], in_=trig[:, m, 1, :], mul=-1.0)
+    nc.scalar.copy(out=rotation[:, 1, 1, :], in_=trig[:, m, 0, :])
+    tables = []
+    for w in range(2):
+        table = keep.tile([P, HEAD_DIM, 2], F32, name="table%d%d" % (m, w))
+        nc.vector.tensor_tensor(
+            out=table[:].rearrange("p (i a) b -> p i a b", a=2),
+            in0=rotation[:].rearrange("p a b i -> p i a b"),
+            in1=gains[:, w, :].rearrange("p (i a) -> p i a", a=2).unsqueeze(3).to_broadcast([P, PAIRS, 2, 2]),
+            op=ALU.mult,
+        )
+        tables.append(table)
+    return tables
 
 
 def tile_flux2parallelselfattention_pa_kernel(
@@ -127,17 +146,18 @@ def tile_flux2parallelselfattention_pa_kernel(
 ):
     nc = tc.nc
     with ExitStack() as ctx:
+        ctx.enter_context(tc.manual_schedule())
         keep = ctx.enter_context(tc.tile_pool(name="keep", bufs=1))
         work = ctx.enter_context(tc.tile_pool(name="work", bufs=3 * TOKEN_TILES * BANKS))
         psum = ctx.enter_context(tc.psum_pool(name="psum", bufs=8))
 
         gain_rows = keep.tile([P, 2, HEAD_DIM], BF16, name="gain_rows")
         nc.vector.memset(gain_rows[:], 0.0)
-        nc.gpsimd.dma_start(out=gain_rows[0:1, 0, :], in_=norm_q_w.unsqueeze(0))
-        nc.gpsimd.dma_start(out=gain_rows[0:1, 1, :], in_=norm_k_w.unsqueeze(0))
+        nc.scalar.dma_start(out=gain_rows[0:1, 0, :], in_=norm_q_w.unsqueeze(0))
+        nc.scalar.dma_start(out=gain_rows[0:1, 1, :], in_=norm_k_w.unsqueeze(0))
         trig = keep.tile([P, TOKEN_TILES, 2, PAIRS], BF16, name="trig")
-        nc.scalar.dma_start(out=trig[:, :, 0, :], in_=cos.rearrange("(m p) i -> p m i", p=P))
-        nc.scalar.dma_start(out=trig[:, :, 1, :], in_=sin.rearrange("(m p) i -> p m i", p=P))
+        nc.gpsimd.dma_start(out=trig[:, :, 0, :], in_=cos.rearrange("(m p) i -> p m i", p=P))
+        nc.gpsimd.dma_start(out=trig[:, :, 1, :], in_=sin.rearrange("(m p) i -> p m i", p=P))
         x_rows = hidden_states.rearrange("b (m p) d -> m p (b d)", p=P)
         x_tiles = [keep.tile([P, D_MODEL], BF16, name="x_sb%d" % m) for m in range(TOKEN_TILES)]
         nc.sync.dma_start(out=x_tiles[0][:], in_=x_rows[0])
@@ -148,48 +168,37 @@ def tile_flux2parallelselfattention_pa_kernel(
 
         identity = keep.tile([P, P], F32, name="identity")
         make_identity(nc, identity[:])
+        ones = keep.tile([P, P], BF16, name="ones")
+        nc.vector.memset(ones[:], 1.0)
 
         one = keep.tile([P, 1], F32, name="one")
         nc.vector.memset(one[:], 1.0)
         warm = keep.tile([P, 1], F32, name="warm")
         nc.scalar.activation(out=warm[:], in_=one[:], func=ACT.Abs_reciprocal_sqrt)
 
-        x_mx = [quantise_tokens(nc, keep, psum, nc.scalar.copy, m, x_tiles[m], identity) for m in range(TOKEN_TILES)]
-
-        rotation = keep.tile([P, TOKEN_TILES, 2, 2, PAIRS], F32, name="rotation")
-        nc.scalar.copy(out=rotation[:, :, 0, :, :], in_=trig[:])
-        nc.scalar.mul(out=rotation[:, :, 1, 0, :], in_=trig[:, :, 1, :], mul=-1.0)
-        nc.scalar.copy(out=rotation[:, :, 1, 1, :], in_=trig[:, :, 0, :])
-        ones = keep.tile([P, P], BF16, name="ones")
-        nc.vector.memset(ones[:], 1.0)
+        x_mx = [quantise_tokens(nc, keep, psum, 0, x_tiles[0], identity)]
         gains = psum.tile([P, 2, HEAD_DIM], F32, name="gains", tag="bank")
         nc.tensor.matmul(out=gains[:], lhsT=ones[:], rhs=gain_rows[:], start=True, stop=True)
-        tables = keep.tile([P, TOKEN_TILES, 2, HEAD_DIM, 2], F32, name="tables")
-        for m in range(TOKEN_TILES):
-            for w in range(2):
-                nc.vector.tensor_tensor(
-                    out=tables[:, m, w].rearrange("p (i a) b -> p i a b", a=2),
-                    in0=rotation[:, m].rearrange("p a b i -> p i a b"),
-                    in1=gains[:, w, :].rearrange("p (i a) -> p i a", a=2).unsqueeze(3).to_broadcast([P, PAIRS, 2, 2]),
-                    op=ALU.mult,
-                )
+        tables = [rotary_tables(nc, keep, m, trig, gains) for m in range(TOKEN_TILES)]
 
         outs = [o.rearrange("b (m p) h d -> m p (b h) d", p=P) for o in (out_0, out_1, out_2)]
         heads = [slice(BANK_HEADS * bank, BANK_HEADS * (bank + 1)) for bank in range(BANKS)]
 
         for m in range(TOKEN_TILES):
-            x_codes, x_scales = x_mx[m]
             for w, (words, planes) in enumerate((weight_q, weight_k)):
                 for bank in range(BANKS):
-                    acc = project(nc, psum, x_codes, x_scales, words, planes, bank)
+                    acc = project(nc, psum, x_mx[m], words, planes, bank)
                     inv_rms = inverse_rms(nc, work, acc)
-                    norm_and_rotate(nc, work, acc, inv_rms, tables[:, m, w], outs[w][m][:, heads[bank], :])
+                    last = (m, w, bank) == (TOKEN_TILES - 1, 1, BANKS - 1)
+                    adder = nc.vector if last else nc.gpsimd
+                    norm_and_rotate(nc, work, adder, acc, inv_rms, tables[m][w][:], outs[w][m][:, heads[bank], :])
+                if w == 0 and m + 1 < TOKEN_TILES:
+                    x_mx.append(quantise_tokens(nc, keep, psum, m + 1, x_tiles[m + 1], identity))
 
         words, planes = weight_v
         for m in range(TOKEN_TILES):
-            x_codes, x_scales = x_mx[m]
             for bank in range(BANKS):
-                acc_v = project(nc, psum, x_codes, x_scales, words, planes, bank)
+                acc_v = project(nc, psum, x_mx[m], words, planes, bank)
                 values = work.tile([P, BANK_HEADS, HEAD_DIM], F32, name="values")
                 nc.scalar.copy(out=values[:].rearrange("p h d -> p (h d)"), in_=acc_v[:])
-                nc.sync.dma_start(out=outs[2][m][:, heads[bank], :], in_=values[:])
+                nc.scalar.dma_start(out=outs[2][m][:, heads[bank], :], in_=values[:])

@@ -33,15 +33,27 @@ WORDS_PER_PASS = K_PASS // 2
 FLOPS = 2 * TOKENS * D_MODEL * 3 * HEADS * HEAD_DIM
 
 
-def load_weight(nc, keep, label, words_in, scales_in):
+def weight_tiles(nc, keep, label):
     words = keep.tile([P, PASSES, 2 * HEADS * HEAD_DIM], U8, name="words_" + label, align_bytes=64)
-    nc.sync.dma_start(out=words[:].bitcast(I32), in_=words_in.rearrange("g p b -> p g b").bitcast(I32))
     planes = keep.tile([P, PASSES, HEADS * HEAD_DIM], U8, name="planes_" + label, align_bytes=64)
     nc.vector.memset(planes[:].bitcast(I32), 0)
+    return words, planes
+
+
+def load_words(nc, weight, words_in, banks):
+    words = weight[0]
+    first = 2 * BANK_COLS * banks[0]
+    last = 2 * BANK_COLS * (banks[-1] + 1)
+    nc.sync.dma_start(
+        out=words[:, :, first:last].bitcast(I32), in_=words_in.rearrange("g p b -> p g b")[:, :, first:last].bitcast(I32)
+    )
+
+
+def load_scales(nc, weight, scales_in):
+    planes = weight[1]
     by_row = scales_in.rearrange("g (quad r) n -> r quad g n", r=4)
     for r in range(4):
         nc.sync.dma_start(out=planes[r:P:32, :, :].bitcast(I32), in_=by_row[r].bitcast(I32))
-    return words, planes
 
 
 def quantise_tokens(nc, keep, psum, m, x_sb, identity):
@@ -155,28 +167,33 @@ def tile_flux2parallelselfattention_pa_kernel(
         nc.vector.memset(gain_rows[:], 0.0)
         nc.scalar.dma_start(out=gain_rows[0:1, 0, :], in_=norm_q_w.unsqueeze(0))
         nc.scalar.dma_start(out=gain_rows[0:1, 1, :], in_=norm_k_w.unsqueeze(0))
-        trig = keep.tile([P, TOKEN_TILES, 2, PAIRS], BF16, name="trig")
-        nc.gpsimd.dma_start(out=trig[:, :, 0, :], in_=cos.rearrange("(m p) i -> p m i", p=P))
-        nc.gpsimd.dma_start(out=trig[:, :, 1, :], in_=sin.rearrange("(m p) i -> p m i", p=P))
+        identity = keep.tile([P, P], F32, name="identity")
+        make_identity(nc, identity[:])
+        weight_q = weight_tiles(nc, keep, "q")
         x_rows = hidden_states.rearrange("b (m p) d -> m p (b d)", p=P)
         x_tiles = [keep.tile([P, D_MODEL], BF16, name="x_sb%d" % m) for m in range(TOKEN_TILES)]
         nc.sync.dma_start(out=x_tiles[0][:], in_=x_rows[0])
-        weight_q = load_weight(nc, keep, "q", w_q_words, w_q_scales)
         nc.sync.dma_start(out=x_tiles[1][:], in_=x_rows[1])
-        weight_k = load_weight(nc, keep, "k", w_k_words, w_k_scales)
-        weight_v = load_weight(nc, keep, "v", w_v_words, w_v_scales)
-
-        identity = keep.tile([P, P], F32, name="identity")
-        make_identity(nc, identity[:])
+        load_words(nc, weight_q, w_q_words, [0])
+        load_scales(nc, weight_q, w_q_scales)
+        trig = keep.tile([P, TOKEN_TILES, 2, PAIRS], BF16, name="trig")
+        nc.sync.dma_start(out=trig[:, :, 0, :], in_=cos.rearrange("(m p) i -> p m i", p=P))
+        nc.sync.dma_start(out=trig[:, :, 1, :], in_=sin.rearrange("(m p) i -> p m i", p=P))
         ones = keep.tile([P, P], BF16, name="ones")
         nc.vector.memset(ones[:], 1.0)
-
         one = keep.tile([P, 1], F32, name="one")
         nc.vector.memset(one[:], 1.0)
         warm = keep.tile([P, 1], F32, name="warm")
         nc.scalar.activation(out=warm[:], in_=one[:], func=ACT.Abs_reciprocal_sqrt)
+        weight_k = weight_tiles(nc, keep, "k")
+        weight_v = weight_tiles(nc, keep, "v")
+        load_words(nc, weight_q, w_q_words, [1])
+        load_words(nc, weight_k, w_k_words, [0, 1])
+        load_scales(nc, weight_k, w_k_scales)
+        load_words(nc, weight_v, w_v_words, [0, 1])
+        load_scales(nc, weight_v, w_v_scales)
 
-        x_mx = [quantise_tokens(nc, keep, psum, 0, x_tiles[0], identity)]
+        x_mx = [quantise_tokens(nc, keep, psum, m, x_tiles[m], identity) for m in range(TOKEN_TILES)]
         gains = psum.tile([P, 2, HEAD_DIM], F32, name="gains", tag="bank")
         nc.tensor.matmul(out=gains[:], lhsT=ones[:], rhs=gain_rows[:], start=True, stop=True)
         tables = [rotary_tables(nc, keep, m, trig, gains) for m in range(TOKEN_TILES)]
@@ -192,8 +209,6 @@ def tile_flux2parallelselfattention_pa_kernel(
                     last = (m, w, bank) == (TOKEN_TILES - 1, 1, BANKS - 1)
                     adder = nc.vector if last else nc.gpsimd
                     norm_and_rotate(nc, work, adder, acc, inv_rms, tables[m][w][:], outs[w][m][:, heads[bank], :])
-                if w == 0 and m + 1 < TOKEN_TILES:
-                    x_mx.append(quantise_tokens(nc, keep, psum, m + 1, x_tiles[m + 1], identity))
 
         words, planes = weight_v
         for m in range(TOKEN_TILES):

@@ -91,12 +91,13 @@ def project(nc, psum, x_mx, words, planes, bank):
     return acc
 
 
-def inverse_rms(nc, work, acc):
-    squares = work.tile([P, BANK_COLS], BF16, name="squares")
-    sum_sq = work.tile([P, BANK_HEADS], F32, name="sum_sq")
-    for h in range(BANK_HEADS):
+def sum_squares(nc, squares, sum_sq, acc, first, last):
+    for h in range(first, last):
         cols = slice(HEAD_DIM * h, HEAD_DIM * (h + 1))
         nc.scalar.activation(out=squares[:, cols], in_=acc[:, cols], func=ACT.Square, accum_out=sum_sq[:, h : h + 1])
+
+
+def inverse_rms(nc, work, sum_sq):
     inv_rms = work.tile([P, BANK_HEADS], F32, name="inv_rms")
     nc.scalar.activation(out=inv_rms[:], in_=sum_sq[:], func=ACT.Abs_reciprocal_sqrt, scale=1.0 / HEAD_DIM, bias=EPS)
     return inv_rms
@@ -201,19 +202,36 @@ def tile_flux2parallelselfattention_pa_kernel(
         outs = [o.rearrange("b (m p) h d -> m p (b h) d", p=P) for o in (out_0, out_1, out_2)]
         heads = [slice(BANK_HEADS * bank, BANK_HEADS * (bank + 1)) for bank in range(BANKS)]
 
-        for m in range(TOKEN_TILES):
-            for w, (words, planes) in enumerate((weight_q, weight_k)):
-                for bank in range(BANKS):
-                    acc = project(nc, psum, x_mx[m], words, planes, bank)
-                    inv_rms = inverse_rms(nc, work, acc)
-                    last = (m, w, bank) == (TOKEN_TILES - 1, 1, BANKS - 1)
-                    adder = nc.vector if last else nc.gpsimd
-                    norm_and_rotate(nc, work, adder, acc, inv_rms, tables[m][w][:], outs[w][m][:, heads[bank], :])
+        order = [(m, w, bank) for m in range(TOKEN_TILES) for w in range(2) for bank in range(BANKS)]
+        last = len(order) - 1
+        accs = []
+        sums = []
 
-        words, planes = weight_v
-        for m in range(TOKEN_TILES):
-            for bank in range(BANKS):
-                acc_v = project(nc, psum, x_mx[m], words, planes, bank)
-                values = work.tile([P, BANK_HEADS, HEAD_DIM], F32, name="values")
-                nc.scalar.copy(out=values[:].rearrange("p h d -> p (h d)"), in_=acc_v[:])
-                nc.scalar.dma_start(out=outs[2][m][:, heads[bank], :], in_=values[:])
+        def finish(n):
+            m, w, bank = order[n]
+            inv_rms = inverse_rms(nc, work, sums[n])
+            adder = nc.vector if n == last else nc.gpsimd
+            norm_and_rotate(nc, work, adder, accs[n], inv_rms, tables[m][w][:], outs[w][m][:, heads[bank], :])
+
+        def values(m, bank):
+            acc_v = project(nc, psum, x_mx[m], weight_v[0], weight_v[1], bank)
+            copied = work.tile([P, BANK_HEADS, HEAD_DIM], F32, name="values")
+            nc.scalar.copy(out=copied[:].rearrange("p h d -> p (h d)"), in_=acc_v[:])
+            nc.scalar.dma_start(out=outs[2][m][:, heads[bank], :], in_=copied[:])
+
+        for n, (m, w, bank) in enumerate(order):
+            words, planes = (weight_q, weight_k)[w]
+            accs.append(project(nc, psum, x_mx[m], words, planes, bank))
+            squares = work.tile([P, BANK_COLS], BF16, name="squares")
+            sums.append(work.tile([P, BANK_HEADS], F32, name="sum_sq"))
+            sum_squares(nc, squares, sums[n], accs[n], 0, 2)
+            if n >= 2:
+                finish(n - 1)
+            sum_squares(nc, squares, sums[n], accs[n], 2, BANK_HEADS)
+            if n == 0:
+                finish(0)
+        values(0, 0)
+        finish(last)
+        values(0, 1)
+        values(1, 0)
+        values(1, 1)

@@ -103,7 +103,7 @@ def inverse_rms(nc, work, sum_sq):
     return inv_rms
 
 
-def norm_and_rotate(nc, work, adder, acc, inv_rms, table, out_rows):
+def norm_and_rotate(nc, work, adder, pieces, acc, inv_rms, table, out_rows):
     products = work.tile([P, BANK_HEADS, HEAD_DIM, 2], F32, name="products")
     for h in range(BANK_HEADS):
         nc.vector.scalar_tensor_tensor(
@@ -114,11 +114,17 @@ def norm_and_rotate(nc, work, adder, acc, inv_rms, table, out_rows):
             op0=ALU.mult,
             op1=ALU.mult,
         )
-    by_feature = products[:].rearrange("p h (i a) b -> p a (h i) b", a=2)
     finished = work.tile([P, BANK_HEADS, HEAD_DIM], F32, name="finished")
-    adder.tensor_tensor(
-        out=finished[:].rearrange("p h (i b) -> p (h i) b", b=2), in0=by_feature[:, 0], in1=by_feature[:, 1], op=ALU.add
-    )
+    step = BANK_HEADS // pieces
+    for first in range(0, BANK_HEADS, step):
+        part = slice(first, first + step)
+        by_feature = products[:, part].rearrange("p h (i a) b -> p a (h i) b", a=2)
+        adder.tensor_tensor(
+            out=finished[:, part].rearrange("p h (i b) -> p (h i) b", b=2),
+            in0=by_feature[:, 0],
+            in1=by_feature[:, 1],
+            op=ALU.add,
+        )
     nc.sync.dma_start(out=out_rows, in_=finished[:])
 
 
@@ -211,13 +217,16 @@ def tile_flux2parallelselfattention_pa_kernel(
             m, w, bank = order[n]
             inv_rms = inverse_rms(nc, work, sums[n])
             adder = nc.vector if n == last else nc.gpsimd
-            norm_and_rotate(nc, work, adder, accs[n], inv_rms, tables[m][w][:], outs[w][m][:, heads[bank], :])
+            pieces = 2 if n == last else 1
+            norm_and_rotate(nc, work, adder, pieces, accs[n], inv_rms, tables[m][w][:], outs[w][m][:, heads[bank], :])
+
+        copied = [work.tile([P, HEADS, HEAD_DIM], F32, name="values") for m in range(TOKEN_TILES)]
 
         def values(m, bank):
             acc_v = project(nc, psum, x_mx[m], weight_v[0], weight_v[1], bank)
-            copied = work.tile([P, BANK_HEADS, HEAD_DIM], F32, name="values")
-            nc.scalar.copy(out=copied[:].rearrange("p h d -> p (h d)"), in_=acc_v[:])
-            nc.scalar.dma_start(out=outs[2][m][:, heads[bank], :], in_=copied[:])
+            nc.scalar.copy(out=copied[m][:, heads[bank], :].rearrange("p h d -> p (h d)"), in_=acc_v[:])
+            if bank == BANKS - 1:
+                nc.scalar.dma_start(out=outs[2][m], in_=copied[m][:])
 
         for n, (m, w, bank) in enumerate(order):
             words, planes = (weight_q, weight_k)[w]

@@ -128,17 +128,13 @@ def norm_and_rotate(nc, work, adder, pieces, acc, inv_rms, table, out_rows):
     nc.sync.dma_start(out=out_rows, in_=finished[:])
 
 
-def rotary_tables(nc, keep, m, trig, gains):
-    rotation = keep.tile([P, 2, 2, PAIRS], F32, name="rotation%d" % m)
-    nc.scalar.copy(out=rotation[:, 0, :, :], in_=trig[:, m, :, :])
-    nc.scalar.mul(out=rotation[:, 1, 0, :], in_=trig[:, m, 1, :], mul=-1.0)
-    nc.scalar.copy(out=rotation[:, 1, 1, :], in_=trig[:, m, 0, :])
+def rotary_tables(nc, keep, m, rotation, gains):
     tables = []
     for w in range(2):
         table = keep.tile([P, HEAD_DIM, 2], F32, name="table%d%d" % (m, w))
         nc.vector.tensor_tensor(
             out=table[:].rearrange("p (i a) b -> p i a b", a=2),
-            in0=rotation[:].rearrange("p a b i -> p i a b"),
+            in0=rotation[:, m].rearrange("p a b i -> p i a b"),
             in1=gains[:, w, :].rearrange("p (i a) -> p i a", a=2).unsqueeze(3).to_broadcast([P, PAIRS, 2, 2]),
             op=ALU.mult,
         )
@@ -183,9 +179,9 @@ def tile_flux2parallelselfattention_pa_kernel(
         nc.sync.dma_start(out=x_tiles[1][:], in_=x_rows[1])
         load_words(nc, weight_q, w_q_words, [0])
         load_scales(nc, weight_q, w_q_scales)
-        trig = keep.tile([P, TOKEN_TILES, 2, PAIRS], BF16, name="trig")
-        nc.sync.dma_start(out=trig[:, :, 0, :], in_=cos.rearrange("(m p) i -> p m i", p=P))
-        nc.sync.dma_start(out=trig[:, :, 1, :], in_=sin.rearrange("(m p) i -> p m i", p=P))
+        rotation = keep.tile([P, TOKEN_TILES, 2, 2, PAIRS], BF16, name="rotation")
+        nc.sync.dma_start(out=rotation[:, :, 0, 0, :], in_=cos.rearrange("(m p) i -> p m i", p=P))
+        nc.sync.dma_start(out=rotation[:, :, 0, 1, :], in_=sin.rearrange("(m p) i -> p m i", p=P))
         ones = keep.tile([P, P], BF16, name="ones")
         nc.vector.memset(ones[:], 1.0)
         one = keep.tile([P, 1], F32, name="one")
@@ -203,7 +199,9 @@ def tile_flux2parallelselfattention_pa_kernel(
         x_mx = [quantise_tokens(nc, keep, psum, m, x_tiles[m], identity) for m in range(TOKEN_TILES)]
         gains = psum.tile([P, 2, HEAD_DIM], F32, name="gains", tag="bank")
         nc.tensor.matmul(out=gains[:], lhsT=ones[:], rhs=gain_rows[:], start=True, stop=True)
-        tables = [rotary_tables(nc, keep, m, trig, gains) for m in range(TOKEN_TILES)]
+        nc.vector.tensor_scalar_mul(out=rotation[:, :, 1, 0, :], in0=rotation[:, :, 0, 1, :], scalar1=-1.0)
+        nc.vector.tensor_copy(out=rotation[:, :, 1, 1, :], in_=rotation[:, :, 0, 0, :])
+        tables = [rotary_tables(nc, keep, m, rotation, gains) for m in range(TOKEN_TILES)]
 
         outs = [o.rearrange("b (m p) h d -> m p (b h) d", p=P) for o in (out_0, out_1, out_2)]
         heads = [slice(BANK_HEADS * bank, BANK_HEADS * (bank + 1)) for bank in range(BANKS)]

@@ -30,22 +30,25 @@ BANK_HEADS = BANK_COLS // HEAD_DIM
 BANKS = HEADS * HEAD_DIM // BANK_COLS
 WORDS_PER_PASS = K_PASS // 2
 
+WARM_UP = 10
+
 FLOPS = 2 * TOKENS * D_MODEL * 3 * HEADS * HEAD_DIM
 
 
 def weight_tiles(nc, keep, label):
-    words = keep.tile([P, PASSES, 2 * HEADS * HEAD_DIM], U8, name="words_" + label, align_bytes=64)
+    words = [
+        keep.tile([P, PASSES, 2 * BANK_COLS], U8, name="words_%s%d" % (label, bank), align_bytes=64)
+        for bank in range(BANKS)
+    ]
     planes = keep.tile([P, PASSES, HEADS * HEAD_DIM], U8, name="planes_" + label, align_bytes=64)
     nc.vector.memset(planes[:].bitcast(I32), 0)
     return words, planes
 
 
-def load_words(nc, weight, words_in, banks):
-    words = weight[0]
-    first = 2 * BANK_COLS * banks[0]
-    last = 2 * BANK_COLS * (banks[-1] + 1)
+def load_words(nc, weight, words_in, bank):
+    cols = slice(2 * BANK_COLS * bank, 2 * BANK_COLS * (bank + 1))
     nc.sync.dma_start(
-        out=words[:, :, first:last].bitcast(I32), in_=words_in.rearrange("g p b -> p g b")[:, :, first:last].bitcast(I32)
+        out=weight[0][bank][:].bitcast(I32), in_=words_in.rearrange("g p b -> p g b")[:, :, cols].bitcast(I32)
     )
 
 
@@ -83,7 +86,7 @@ def project(nc, psum, x_mx, words, planes, bank):
             out=acc[:],
             lhsT=x_codes[:].bitcast(FP8X4),
             lhsT_scale=x_scales[:],
-            rhs=words[:, g, 2 * BANK_COLS * bank : 2 * BANK_COLS * (bank + 1)].bitcast(FP4X4),
+            rhs=words[bank][:, g, :].bitcast(FP4X4),
             rhs_scale=planes[:, g, BANK_COLS * bank : BANK_COLS * (bank + 1)],
             start=(g == 0),
             stop=(g == PASSES - 1),
@@ -166,42 +169,45 @@ def tile_flux2parallelselfattention_pa_kernel(
         work = ctx.enter_context(tc.tile_pool(name="work", bufs=3 * TOKEN_TILES * BANKS))
         psum = ctx.enter_context(tc.psum_pool(name="psum", bufs=8))
 
-        gain_rows = keep.tile([P, 2, HEAD_DIM], BF16, name="gain_rows")
-        nc.vector.memset(gain_rows[:], 0.0)
-        nc.scalar.dma_start(out=gain_rows[0:1, 0, :], in_=norm_q_w.unsqueeze(0))
-        nc.scalar.dma_start(out=gain_rows[0:1, 1, :], in_=norm_k_w.unsqueeze(0))
         identity = keep.tile([P, P], F32, name="identity")
         make_identity(nc, identity[:])
         weight_q = weight_tiles(nc, keep, "q")
-        x_rows = hidden_states.rearrange("b (m p) d -> m p (b d)", p=P)
-        x_tiles = [keep.tile([P, D_MODEL], BF16, name="x_sb%d" % m) for m in range(TOKEN_TILES)]
-        nc.sync.dma_start(out=x_tiles[0][:], in_=x_rows[0])
-        nc.sync.dma_start(out=x_tiles[1][:], in_=x_rows[1])
-        load_words(nc, weight_q, w_q_words, [0])
-        load_scales(nc, weight_q, w_q_scales)
-        rotation = keep.tile([P, TOKEN_TILES, 2, 2, PAIRS], BF16, name="rotation")
-        nc.sync.dma_start(out=rotation[:, :, 0, 0, :], in_=cos.rearrange("(m p) i -> p m i", p=P))
-        nc.sync.dma_start(out=rotation[:, :, 0, 1, :], in_=sin.rearrange("(m p) i -> p m i", p=P))
         ones = keep.tile([P, P], BF16, name="ones")
         nc.vector.memset(ones[:], 1.0)
+        idle = psum.tile([P, P], F32, name="idle", tag="bank")
+        for i in range(WARM_UP):
+            nc.tensor.matmul(out=idle[:], lhsT=ones[:], rhs=ones[:], start=True, stop=True)
         one = keep.tile([P, 1], F32, name="one")
         nc.vector.memset(one[:], 1.0)
         warm = keep.tile([P, 1], F32, name="warm")
         nc.scalar.activation(out=warm[:], in_=one[:], func=ACT.Abs_reciprocal_sqrt)
+        x_rows = hidden_states.rearrange("b (m p) d -> m p (b d)", p=P)
+        x_tiles = [keep.tile([P, D_MODEL], BF16, name="x_sb%d" % m) for m in range(TOKEN_TILES)]
+        nc.sync.dma_start(out=x_tiles[0][:], in_=x_rows[0])
+        nc.sync.dma_start(out=x_tiles[1][:], in_=x_rows[1])
+        load_scales(nc, weight_q, w_q_scales)
+        load_words(nc, weight_q, w_q_words, 0)
+        rotation = keep.tile([P, TOKEN_TILES, 2, 2, PAIRS], BF16, name="rotation")
+        nc.sync.dma_start(out=rotation[:, :, 0, 0, :], in_=cos.rearrange("(m p) i -> p m i", p=P))
+        nc.sync.dma_start(out=rotation[:, :, 0, 1, :], in_=sin.rearrange("(m p) i -> p m i", p=P))
+        gain_rows = keep.tile([P, 2, HEAD_DIM], BF16, name="gain_rows")
+        nc.vector.memset(gain_rows[:], 0.0)
+        nc.sync.dma_start(out=gain_rows[0:1, 0, :], in_=norm_q_w.unsqueeze(0))
+        nc.sync.dma_start(out=gain_rows[0:1, 1, :], in_=norm_k_w.unsqueeze(0))
         weight_k = weight_tiles(nc, keep, "k")
         weight_v = weight_tiles(nc, keep, "v")
-        load_words(nc, weight_q, w_q_words, [1])
-        load_words(nc, weight_k, w_k_words, [0, 1])
+        load_words(nc, weight_q, w_q_words, 1)
+        load_words(nc, weight_k, w_k_words, 0)
         load_scales(nc, weight_k, w_k_scales)
-        load_words(nc, weight_v, w_v_words, [0, 1])
+        load_words(nc, weight_k, w_k_words, 1)
+        load_words(nc, weight_v, w_v_words, 0)
+        load_words(nc, weight_v, w_v_words, 1)
         load_scales(nc, weight_v, w_v_scales)
 
         x_mx = [quantise_tokens(nc, keep, psum, m, x_tiles[m], identity) for m in range(TOKEN_TILES)]
-        gains = psum.tile([P, 2, HEAD_DIM], F32, name="gains", tag="bank")
-        nc.tensor.matmul(out=gains[:], lhsT=ones[:], rhs=gain_rows[:], start=True, stop=True)
         nc.vector.tensor_scalar_mul(out=rotation[:, :, 1, 0, :], in0=rotation[:, :, 0, 1, :], scalar1=-1.0)
         nc.vector.tensor_copy(out=rotation[:, :, 1, 1, :], in_=rotation[:, :, 0, 0, :])
-        tables = [rotary_tables(nc, keep, m, rotation, gains) for m in range(TOKEN_TILES)]
+        tables = []
 
         outs = [o.rearrange("b (m p) h d -> m p (b h) d", p=P) for o in (out_0, out_1, out_2)]
         heads = [slice(BANK_HEADS * bank, BANK_HEADS * (bank + 1)) for bank in range(BANKS)]
@@ -229,6 +235,10 @@ def tile_flux2parallelselfattention_pa_kernel(
         for n, (m, w, bank) in enumerate(order):
             words, planes = (weight_q, weight_k)[w]
             accs.append(project(nc, psum, x_mx[m], words, planes, bank))
+            if n == 0:
+                gains = psum.tile([P, 2, HEAD_DIM], F32, name="gains", tag="bank")
+                nc.tensor.matmul(out=gains[:], lhsT=ones[:], rhs=gain_rows[:], start=True, stop=True)
+                tables.extend(rotary_tables(nc, keep, tile, rotation, gains) for tile in range(TOKEN_TILES))
             squares = work.tile([P, BANK_COLS], BF16, name="squares")
             sums.append(work.tile([P, BANK_HEADS], F32, name="sum_sq"))
             sum_squares(nc, squares, sums[n], accs[n], 0, 2)

@@ -94,16 +94,44 @@ def project(nc, psum, x_mx, words, planes, bank):
     return acc
 
 
+def by_head(acc):
+    return [acc[:, HEAD_DIM * h : HEAD_DIM * (h + 1)] for h in range(BANK_HEADS)]
+
+
+def project_pair(nc, psum, x_mx, words, planes, bank, pair):
+    heads = []
+    acc = psum.tile([P, 2, HEAD_DIM], F32, name="acc_pair", tag="bank")
+    for h in range(2 * pair, 2 * pair + 2):
+        first = BANK_COLS * bank + HEAD_DIM * h
+        for g in range(PASSES):
+            x_codes, x_scales = x_mx[g]
+            nc.tensor.matmul_mx(
+                out=acc[:, h % 2, :],
+                lhsT=x_codes[:].bitcast(FP8X4),
+                lhsT_scale=x_scales[:],
+                rhs=words[bank][:, g, 2 * HEAD_DIM * h : 2 * HEAD_DIM * (h + 1)].bitcast(FP4X4),
+                rhs_scale=planes[:, g, first : first + HEAD_DIM],
+                start=(g == 0),
+                stop=(g == PASSES - 1),
+            )
+        heads.append(acc[:, h % 2, :])
+    return heads
+
+
 def sum_squares(nc, squares, sum_sq, acc, first, last):
     for h in range(first, last):
         cols = slice(HEAD_DIM * h, HEAD_DIM * (h + 1))
-        nc.scalar.activation(out=squares[:, cols], in_=acc[:, cols], func=ACT.Square, accum_out=sum_sq[:, h : h + 1])
+        nc.scalar.activation(out=squares[:, cols], in_=acc[h], func=ACT.Square, accum_out=sum_sq[:, h : h + 1])
 
 
-def inverse_rms(nc, work, sum_sq):
-    inv_rms = work.tile([P, BANK_HEADS], F32, name="inv_rms")
-    nc.scalar.activation(out=inv_rms[:], in_=sum_sq[:], func=ACT.Abs_reciprocal_sqrt, scale=1.0 / HEAD_DIM, bias=EPS)
-    return inv_rms
+def inverse_rms(nc, inv_rms, sum_sq, first, last):
+    nc.scalar.activation(
+        out=inv_rms[:, first:last],
+        in_=sum_sq[:, first:last],
+        func=ACT.Abs_reciprocal_sqrt,
+        scale=1.0 / HEAD_DIM,
+        bias=EPS,
+    )
 
 
 def norm_and_rotate(nc, work, adder, pieces, acc, inv_rms, table, out_rows):
@@ -111,7 +139,7 @@ def norm_and_rotate(nc, work, adder, pieces, acc, inv_rms, table, out_rows):
     for h in range(BANK_HEADS):
         nc.vector.scalar_tensor_tensor(
             out=products[:, h],
-            in0=acc[:, HEAD_DIM * h : HEAD_DIM * (h + 1)].unsqueeze(2).to_broadcast([P, HEAD_DIM, 2]),
+            in0=acc[h].unsqueeze(2).to_broadcast([P, HEAD_DIM, 2]),
             scalar=inv_rms[:, h : h + 1],
             in1=table,
             op0=ALU.mult,
@@ -131,18 +159,21 @@ def norm_and_rotate(nc, work, adder, pieces, acc, inv_rms, table, out_rows):
     nc.sync.dma_start(out=out_rows, in_=finished[:])
 
 
-def rotary_tables(nc, keep, m, rotation, gains):
-    tables = []
-    for w in range(2):
-        table = keep.tile([P, HEAD_DIM, 2], F32, name="table%d%d" % (m, w))
-        nc.vector.tensor_tensor(
-            out=table[:].rearrange("p (i a) b -> p i a b", a=2),
-            in0=rotation[:, m].rearrange("p a b i -> p i a b"),
-            in1=gains[:, w, :].rearrange("p (i a) -> p i a", a=2).unsqueeze(3).to_broadcast([P, PAIRS, 2, 2]),
-            op=ALU.mult,
-        )
-        tables.append(table)
-    return tables
+def spread_gain(nc, psum, ones, gain_row):
+    gain = psum.tile([P, HEAD_DIM], F32, name="gain", tag="bank")
+    nc.tensor.matmul(out=gain[:], lhsT=ones[:], rhs=gain_row[:], start=True, stop=True)
+    return gain
+
+
+def rotary_table(builder, keep, m, w, rotation, gain):
+    table = keep.tile([P, HEAD_DIM, 2], F32, name="table%d%d" % (m, w))
+    builder.tensor_tensor(
+        out=table[:].rearrange("p (i a) b -> p i a b", a=2),
+        in0=rotation[:, m].rearrange("p a b i -> p i a b"),
+        in1=gain[:].rearrange("p (i a) -> p i a", a=2).unsqueeze(3).to_broadcast([P, PAIRS, 2, 2]),
+        op=ALU.mult,
+    )
+    return table
 
 
 def tile_flux2parallelselfattention_pa_kernel(
@@ -171,9 +202,12 @@ def tile_flux2parallelselfattention_pa_kernel(
 
         identity = keep.tile([P, P], F32, name="identity")
         make_identity(nc, identity[:])
-        weight_q = weight_tiles(nc, keep, "q")
+        gain_rows = [keep.tile([P, HEAD_DIM], BF16, name="gain_row%d" % w) for w in range(2)]
+        nc.vector.memset(gain_rows[0][:], 0.0)
+        nc.gpsimd.dma_start(out=gain_rows[0][0:1, :], in_=norm_q_w.unsqueeze(0))
         ones = keep.tile([P, P], BF16, name="ones")
         nc.vector.memset(ones[:], 1.0)
+        weight_q = weight_tiles(nc, keep, "q")
         idle = psum.tile([P, P], F32, name="idle", tag="bank")
         for i in range(WARM_UP):
             nc.tensor.matmul(out=idle[:], lhsT=ones[:], rhs=ones[:], start=True, stop=True)
@@ -183,20 +217,20 @@ def tile_flux2parallelselfattention_pa_kernel(
         nc.scalar.activation(out=warm[:], in_=one[:], func=ACT.Abs_reciprocal_sqrt)
         x_rows = hidden_states.rearrange("b (m p) d -> m p (b d)", p=P)
         x_tiles = [keep.tile([P, D_MODEL], BF16, name="x_sb%d" % m) for m in range(TOKEN_TILES)]
-        nc.sync.dma_start(out=x_tiles[0][:], in_=x_rows[0])
+        for g in range(PASSES):
+            cols = slice(K_PASS * g, K_PASS * (g + 1))
+            nc.sync.dma_start(out=x_tiles[0][:, cols], in_=x_rows[0][:, cols])
         nc.sync.dma_start(out=x_tiles[1][:], in_=x_rows[1])
-        load_scales(nc, weight_q, w_q_scales)
         load_words(nc, weight_q, w_q_words, 0)
+        load_scales(nc, weight_q, w_q_scales)
         rotation = keep.tile([P, TOKEN_TILES, 2, 2, PAIRS], BF16, name="rotation")
         nc.sync.dma_start(out=rotation[:, :, 0, 0, :], in_=cos.rearrange("(m p) i -> p m i", p=P))
         nc.sync.dma_start(out=rotation[:, :, 0, 1, :], in_=sin.rearrange("(m p) i -> p m i", p=P))
-        gain_rows = keep.tile([P, 2, HEAD_DIM], BF16, name="gain_rows")
-        nc.vector.memset(gain_rows[:], 0.0)
-        nc.sync.dma_start(out=gain_rows[0:1, 0, :], in_=norm_q_w.unsqueeze(0))
-        nc.sync.dma_start(out=gain_rows[0:1, 1, :], in_=norm_k_w.unsqueeze(0))
+        load_words(nc, weight_q, w_q_words, 1)
+        nc.vector.memset(gain_rows[1][:], 0.0)
+        nc.sync.dma_start(out=gain_rows[1][0:1, :], in_=norm_k_w.unsqueeze(0))
         weight_k = weight_tiles(nc, keep, "k")
         weight_v = weight_tiles(nc, keep, "v")
-        load_words(nc, weight_q, w_q_words, 1)
         load_words(nc, weight_k, w_k_words, 0)
         load_scales(nc, weight_k, w_k_scales)
         load_words(nc, weight_k, w_k_words, 1)
@@ -207,8 +241,6 @@ def tile_flux2parallelselfattention_pa_kernel(
         x_mx = [quantise_tokens(nc, keep, psum, m, x_tiles[m], identity) for m in range(TOKEN_TILES)]
         nc.vector.tensor_scalar_mul(out=rotation[:, :, 1, 0, :], in0=rotation[:, :, 0, 1, :], scalar1=-1.0)
         nc.vector.tensor_copy(out=rotation[:, :, 1, 1, :], in_=rotation[:, :, 0, 0, :])
-        tables = []
-
         outs = [o.rearrange("b (m p) h d -> m p (b h) d", p=P) for o in (out_0, out_1, out_2)]
         heads = [slice(BANK_HEADS * bank, BANK_HEADS * (bank + 1)) for bank in range(BANKS)]
 
@@ -216,13 +248,13 @@ def tile_flux2parallelselfattention_pa_kernel(
         last = len(order) - 1
         accs = []
         sums = []
+        factors = []
 
         def finish(n):
             m, w, bank = order[n]
-            inv_rms = inverse_rms(nc, work, sums[n])
             adder = nc.vector if n == last else nc.gpsimd
             pieces = 2 if n == last else 1
-            norm_and_rotate(nc, work, adder, pieces, accs[n], inv_rms, tables[m][w][:], outs[w][m][:, heads[bank], :])
+            norm_and_rotate(nc, work, adder, pieces, accs[n], factors[n], tables[(m, w)][:], outs[w][m][:, heads[bank], :])
 
         copied = [work.tile([P, HEADS, HEAD_DIM], F32, name="values") for m in range(TOKEN_TILES)]
 
@@ -234,21 +266,31 @@ def tile_flux2parallelselfattention_pa_kernel(
 
         for n, (m, w, bank) in enumerate(order):
             words, planes = (weight_q, weight_k)[w]
-            accs.append(project(nc, psum, x_mx[m], words, planes, bank))
             if n == 0:
-                gains = psum.tile([P, 2, HEAD_DIM], F32, name="gains", tag="bank")
-                nc.tensor.matmul(out=gains[:], lhsT=ones[:], rhs=gain_rows[:], start=True, stop=True)
-                tables.extend(rotary_tables(nc, keep, tile, rotation, gains) for tile in range(TOKEN_TILES))
+                accs.append(project_pair(nc, psum, x_mx[m], words, planes, bank, 0))
+                gain_q = spread_gain(nc, psum, ones, gain_rows[0])
+                accs[0].extend(project_pair(nc, psum, x_mx[m], words, planes, bank, 1))
+                tables = {(0, 0): rotary_table(nc.vector, keep, 0, 0, rotation, gain_q)}
+                gain_q_sb = keep.tile([P, HEAD_DIM], F32, name="gain_q_sb")
+                nc.vector.tensor_copy(out=gain_q_sb[:], in_=gain_q[:])
+                tables[(1, 0)] = rotary_table(nc.gpsimd, keep, 1, 0, rotation, gain_q_sb)
+            else:
+                accs.append(by_head(project(nc, psum, x_mx[m], words, planes, bank)))
             squares = work.tile([P, BANK_COLS], BF16, name="squares")
             sums.append(work.tile([P, BANK_HEADS], F32, name="sum_sq"))
+            factors.append(work.tile([P, BANK_HEADS], F32, name="inv_rms"))
             sum_squares(nc, squares, sums[n], accs[n], 0, 2)
-            if n >= 2:
-                finish(n - 1)
-            sum_squares(nc, squares, sums[n], accs[n], 2, BANK_HEADS)
             if n == 0:
-                finish(0)
-        values(0, 0)
-        finish(last)
+                inverse_rms(nc, factors[n], sums[n], 0, 2)
+            sum_squares(nc, squares, sums[n], accs[n], 2, BANK_HEADS)
+            inverse_rms(nc, factors[n], sums[n], 2 if n == 0 else 0, BANK_HEADS)
+            if n == 1:
+                gain_k = spread_gain(nc, psum, ones, gain_rows[1])
+                for tile in range(TOKEN_TILES):
+                    tables[(tile, 1)] = rotary_table(nc.vector, keep, tile, 1, rotation, gain_k)
+            if n == last:
+                values(0, 0)
+            finish(n)
         values(0, 1)
         values(1, 0)
         values(1, 1)

@@ -31,6 +31,7 @@ BANKS = HEADS * HEAD_DIM // BANK_COLS
 WORDS_PER_PASS = K_PASS // 2
 
 WARM_UP = 10
+DIRECT = 3
 
 FLOPS = 2 * TOKENS * D_MODEL * 3 * HEADS * HEAD_DIM
 
@@ -202,12 +203,13 @@ def tile_flux2parallelselfattention_pa_kernel(
 
         identity = keep.tile([P, P], F32, name="identity")
         make_identity(nc, identity[:])
-        gain_rows = [keep.tile([P, HEAD_DIM], BF16, name="gain_row%d" % w) for w in range(2)]
-        nc.vector.memset(gain_rows[0][:], 0.0)
-        nc.gpsimd.dma_start(out=gain_rows[0][0:1, :], in_=norm_q_w.unsqueeze(0))
+        weight_q = weight_tiles(nc, keep, "q")
         ones = keep.tile([P, P], BF16, name="ones")
         nc.vector.memset(ones[:], 1.0)
-        weight_q = weight_tiles(nc, keep, "q")
+        gain_rows = [keep.tile([P, HEAD_DIM], BF16, name="gain_row%d" % w) for w in range(2)]
+        for w in range(2):
+            nc.gpsimd.memset(gain_rows[w][:], 0.0)
+        nc.gpsimd.dma_start(out=gain_rows[0][0:1, :], in_=norm_q_w.unsqueeze(0))
         idle = psum.tile([P, P], F32, name="idle", tag="bank")
         for i in range(WARM_UP):
             nc.tensor.matmul(out=idle[:], lhsT=ones[:], rhs=ones[:], start=True, stop=True)
@@ -221,13 +223,12 @@ def tile_flux2parallelselfattention_pa_kernel(
             cols = slice(K_PASS * g, K_PASS * (g + 1))
             nc.sync.dma_start(out=x_tiles[0][:, cols], in_=x_rows[0][:, cols])
         nc.sync.dma_start(out=x_tiles[1][:], in_=x_rows[1])
-        load_words(nc, weight_q, w_q_words, 0)
         load_scales(nc, weight_q, w_q_scales)
+        load_words(nc, weight_q, w_q_words, 0)
         rotation = keep.tile([P, TOKEN_TILES, 2, 2, PAIRS], BF16, name="rotation")
         nc.sync.dma_start(out=rotation[:, :, 0, 0, :], in_=cos.rearrange("(m p) i -> p m i", p=P))
         nc.sync.dma_start(out=rotation[:, :, 0, 1, :], in_=sin.rearrange("(m p) i -> p m i", p=P))
         load_words(nc, weight_q, w_q_words, 1)
-        nc.vector.memset(gain_rows[1][:], 0.0)
         nc.sync.dma_start(out=gain_rows[1][0:1, :], in_=norm_k_w.unsqueeze(0))
         weight_k = weight_tiles(nc, keep, "k")
         weight_v = weight_tiles(nc, keep, "v")
@@ -267,9 +268,11 @@ def tile_flux2parallelselfattention_pa_kernel(
         for n, (m, w, bank) in enumerate(order):
             words, planes = (weight_q, weight_k)[w]
             if n == 0:
-                accs.append(project_pair(nc, psum, x_mx[m], words, planes, bank, 0))
+                accs.append(
+                    project_pair(nc, psum, x_mx[m], words, planes, bank, 0)
+                    + project_pair(nc, psum, x_mx[m], words, planes, bank, 1)
+                )
                 gain_q = spread_gain(nc, psum, ones, gain_rows[0])
-                accs[0].extend(project_pair(nc, psum, x_mx[m], words, planes, bank, 1))
                 tables = {(0, 0): rotary_table(nc.vector, keep, 0, 0, rotation, gain_q)}
                 gain_q_sb = keep.tile([P, HEAD_DIM], F32, name="gain_q_sb")
                 nc.vector.tensor_copy(out=gain_q_sb[:], in_=gain_q[:])
@@ -282,15 +285,21 @@ def tile_flux2parallelselfattention_pa_kernel(
             sum_squares(nc, squares, sums[n], accs[n], 0, 2)
             if n == 0:
                 inverse_rms(nc, factors[n], sums[n], 0, 2)
+            elif n > DIRECT:
+                inverse_rms(nc, factors[n - 1], sums[n - 1], 0, BANK_HEADS)
+                finish(n - 1)
             sum_squares(nc, squares, sums[n], accs[n], 2, BANK_HEADS)
-            inverse_rms(nc, factors[n], sums[n], 2 if n == 0 else 0, BANK_HEADS)
+            if n < DIRECT:
+                inverse_rms(nc, factors[n], sums[n], 2 if n == 0 else 0, BANK_HEADS)
             if n == 1:
                 gain_k = spread_gain(nc, psum, ones, gain_rows[1])
                 for tile in range(TOKEN_TILES):
                     tables[(tile, 1)] = rotary_table(nc.vector, keep, tile, 1, rotation, gain_k)
-            if n == last:
-                values(0, 0)
-            finish(n)
+            if n < DIRECT:
+                finish(n)
+        values(0, 0)
+        inverse_rms(nc, factors[last], sums[last], 0, BANK_HEADS)
+        finish(last)
         values(0, 1)
         values(1, 0)
         values(1, 1)

@@ -135,7 +135,7 @@ def inverse_rms(nc, inv_rms, sum_sq, first, last):
     )
 
 
-def norm_and_rotate(nc, work, adder, pieces, acc, inv_rms, table, out_rows):
+def norm_and_rotate(nc, work, adder, pieces, acc, inv_rms, table):
     products = work.tile([P, BANK_HEADS, HEAD_DIM, 2], F32, name="products")
     for h in range(BANK_HEADS):
         nc.vector.scalar_tensor_tensor(
@@ -157,7 +157,7 @@ def norm_and_rotate(nc, work, adder, pieces, acc, inv_rms, table, out_rows):
             in1=by_feature[:, 1],
             op=ALU.add,
         )
-    nc.sync.dma_start(out=out_rows, in_=finished[:])
+    return finished
 
 
 def spread_gain(nc, psum, ones, gain_row):
@@ -255,7 +255,10 @@ def tile_flux2parallelselfattention_pa_kernel(
             m, w, bank = order[n]
             adder = nc.vector if n == last else nc.gpsimd
             pieces = 2 if n == last else 1
-            norm_and_rotate(nc, work, adder, pieces, accs[n], factors[n], tables[(m, w)][:], outs[w][m][:, heads[bank], :])
+            finished = norm_and_rotate(nc, work, adder, pieces, accs[n], factors[n], tables[(m, w)][:])
+            if n < last:
+                nc.sync.dma_start(out=outs[w][m][:, heads[bank], :], in_=finished[:])
+            return finished
 
         copied = [work.tile([P, HEADS, HEAD_DIM], F32, name="values") for m in range(TOKEN_TILES)]
 
@@ -297,9 +300,10 @@ def tile_flux2parallelselfattention_pa_kernel(
                     tables[(tile, 1)] = rotary_table(nc.vector, keep, tile, 1, rotation, gain_k)
             if n < DIRECT:
                 finish(n)
-        values(0, 0)
         inverse_rms(nc, factors[last], sums[last], 0, BANK_HEADS)
-        finish(last)
+        values(0, 0)
+        last_finished = finish(last)
         values(0, 1)
         values(1, 0)
         values(1, 1)
+        nc.scalar.dma_start(out=outs[1][TOKEN_TILES - 1][:, heads[BANKS - 1], :], in_=last_finished[:])

@@ -30,7 +30,7 @@ BANK_HEADS = BANK_COLS // HEAD_DIM
 BANKS = HEADS * HEAD_DIM // BANK_COLS
 WORDS_PER_PASS = K_PASS // 2
 
-WARM_UP = 10
+WARM_UP = 16
 DIRECT = 3
 
 FLOPS = 2 * TOKENS * D_MODEL * 3 * HEADS * HEAD_DIM
@@ -203,9 +203,9 @@ def tile_flux2parallelselfattention_pa_kernel(
 
         identity = keep.tile([P, P], F32, name="identity")
         make_identity(nc, identity[:])
-        weight_q = weight_tiles(nc, keep, "q")
         ones = keep.tile([P, P], BF16, name="ones")
         nc.vector.memset(ones[:], 1.0)
+        weight_q = weight_tiles(nc, keep, "q")
         gain_rows = [keep.tile([P, HEAD_DIM], BF16, name="gain_row%d" % w) for w in range(2)]
         for w in range(2):
             nc.gpsimd.memset(gain_rows[w][:], 0.0)

from contextlib import ExitStack

import concourse.mybir as mybir
from concourse.masks import make_identity

F32 = mybir.dt.float32
BF16 = mybir.dt.bfloat16
I32 = mybir.dt.int32
U32 = mybir.dt.uint32
U8 = mybir.dt.uint8
FP8X4 = mybir.dt.float8_e4m3fn_x4
FP4X4 = mybir.dt.float4_e2m1fn_x4
ACT = mybir.ActivationFunctionType
ALU = mybir.AluOpType

P = 128
PACK = 4
K_PASS = P * PACK
TOKENS = 256
D_MODEL = 1024
HEADS = 8
HEAD_DIM = 128
PAIRS = HEAD_DIM // 2
EPS = 1e-5

PASSES = D_MODEL // K_PASS
TOKEN_TILES = TOKENS // P
BANK_COLS = 512
BANK_HEADS = BANK_COLS // HEAD_DIM
BANKS = HEADS * HEAD_DIM // BANK_COLS
WORDS_PER_PASS = K_PASS // 2

WARM_UP = 16
DIRECT = 3

FLOPS = 2 * TOKENS * D_MODEL * 3 * HEADS * HEAD_DIM


def weight_tiles(nc, keep, label):
    words = [
        keep.tile([P, PASSES, 2 * BANK_COLS], U8, name="words_%s%d" % (label, bank), align_bytes=64)
        for bank in range(BANKS)
    ]
    planes = keep.tile([P, PASSES, HEADS * HEAD_DIM], U8, name="planes_" + label, align_bytes=64)
    nc.vector.memset(planes[:].bitcast(I32), 0)
    return words, planes


def load_words(nc, weight, words_in, bank):
    cols = slice(2 * BANK_COLS * bank, 2 * BANK_COLS * (bank + 1))
    nc.sync.dma_start(
        out=weight[0][bank][:].bitcast(I32), in_=words_in.rearrange("g p b -> p g b")[:, :, cols].bitcast(I32)
    )


def load_scales(nc, weight, scales_in):
    planes = weight[1]
    by_row = scales_in.rearrange("g (quad r) n -> r quad g n", r=4)
    for r in range(4):
        nc.sync.dma_start(out=planes[r:P:32, :, :].bitcast(I32), in_=by_row[r].bitcast(I32))


def quantise_tokens(nc, keep, psum, m, x_sb, identity):
    x_words = x_sb[:].bitcast(F32)
    quantised = []
    for g in range(PASSES):
        flipped = psum.tile([P, 2, P], F32, name="flipped", tag="bank")
        for u in range(2):
            first = WORDS_PER_PASS * g + u
            nc.tensor.transpose(flipped[:, u, :], x_words[:, first : WORDS_PER_PASS * (g + 1) : 2], identity[:])
        grouped = keep.tile([P, P, PACK], BF16, name="grouped%d%d" % (m, g), align_bytes=64)
        nc.scalar.copy(out=grouped[:].bitcast(F32), in_=flipped[:].rearrange("p u r -> p r u"))
        codes = keep.tile([P, P], U32, name="x_codes%d%d" % (m, g), align_bytes=64)
        scales = keep.tile([P, P], U8, name="x_scales%d%d" % (m, g), align_bytes=64)
        nc.vector.quantize_mx(
            out=codes[:].bitcast(FP8X4), scales=scales[:], in_=grouped[:].rearrange("p r t -> p (r t)")
        )
        quantised.append((codes, scales))
    return quantised


def project(nc, psum, x_mx, words, planes, bank):
    acc = psum.tile([P, BANK_COLS], F32, name="acc", tag="bank")
    for g in range(PASSES):
        x_codes, x_scales = x_mx[g]
        nc.tensor.matmul_mx(
            out=acc[:],
            lhsT=x_codes[:].bitcast(FP8X4),
            lhsT_scale=x_scales[:],
            rhs=words[bank][:, g, :].bitcast(FP4X4),
            rhs_scale=planes[:, g, BANK_COLS * bank : BANK_COLS * (bank + 1)],
            start=(g == 0),
            stop=(g == PASSES - 1),
        )
    return acc


def by_head(acc):
    return [acc[:, HEAD_DIM * h : HEAD_DIM * (h + 1)] for h in range(BANK_HEADS)]


def project_pair(nc, psum, x_mx, words, planes, bank, pair):
    heads = []
    acc = psum.tile([P, 2, HEAD_DIM], F32, name="acc_pair", tag="bank")
    for h in range(2 * pair, 2 * pair + 2):
        first = BANK_COLS * bank + HEAD_DIM * h
        for g in range(PASSES):
            x_codes, x_scales = x_mx[g]
            nc.tensor.matmul_mx(
                out=acc[:, h % 2, :],
                lhsT=x_codes[:].bitcast(FP8X4),
                lhsT_scale=x_scales[:],
                rhs=words[bank][:, g, 2 * HEAD_DIM * h : 2 * HEAD_DIM * (h + 1)].bitcast(FP4X4),
                rhs_scale=planes[:, g, first : first + HEAD_DIM],
                start=(g == 0),
                stop=(g == PASSES - 1),
            )
        heads.append(acc[:, h % 2, :])
    return heads


def sum_squares(nc, squares, sum_sq, acc, first, last):
    for h in range(first, last):
        cols = slice(HEAD_DIM * h, HEAD_DIM * (h + 1))
        nc.scalar.activation(out=squares[:, cols], in_=acc[h], func=ACT.Square, accum_out=sum_sq[:, h : h + 1])


def inverse_rms(nc, inv_rms, sum_sq, first, last):
    nc.scalar.activation(
        out=inv_rms[:, first:last],
        in_=sum_sq[:, first:last],
        func=ACT.Abs_reciprocal_sqrt,
        scale=1.0 / HEAD_DIM,
        bias=EPS,
    )


def norm_and_rotate(nc, work, adder, pieces, acc, inv_rms, table):
    products = work.tile([P, BANK_HEADS, HEAD_DIM, 2], F32, name="products")
    for h in range(BANK_HEADS):
        nc.vector.scalar_tensor_tensor(
            out=products[:, h],
            in0=acc[h].unsqueeze(2).to_broadcast([P, HEAD_DIM, 2]),
            scalar=inv_rms[:, h : h + 1],
            in1=table,
            op0=ALU.mult,
            op1=ALU.mult,
        )
    finished = work.tile([P, BANK_HEADS, HEAD_DIM], F32, name="finished")
    step = BANK_HEADS // pieces
    for first in range(0, BANK_HEADS, step):
        part = slice(first, first + step)
        by_feature = products[:, part].rearrange("p h (i a) b -> p a (h i) b", a=2)
        adder.tensor_tensor(
            out=finished[:, part].rearrange("p h (i b) -> p (h i) b", b=2),
            in0=by_feature[:, 0],
            in1=by_feature[:, 1],
            op=ALU.add,
        )
    return finished


def spread_gain(nc, psum, ones, gain_row):
    gain = psum.tile([P, HEAD_DIM], F32, name="gain", tag="bank")
    nc.tensor.matmul(out=gain[:], lhsT=ones[:], rhs=gain_row[:], start=True, stop=True)
    return gain


def rotary_table(builder, keep, m, w, rotation, gain):
    table = keep.tile([P, HEAD_DIM, 2], F32, name="table%d%d" % (m, w))
    builder.tensor_tensor(
        out=table[:].rearrange("p (i a) b -> p i a b", a=2),
        in0=rotation[:, m].rearrange("p a b i -> p i a b"),
        in1=gain[:].rearrange("p (i a) -> p i a", a=2).unsqueeze(3).to_broadcast([P, PAIRS, 2, 2]),
        op=ALU.mult,
    )
    return table


def tile_flux2parallelselfattention_pa_kernel(
    tc,
    hidden_states,
    w_q_words,
    w_q_scales,
    w_k_words,
    w_k_scales,
    w_v_words,
    w_v_scales,
    norm_q_w,
    norm_k_w,
    cos,
    sin,
    out_0,
    out_1,
    out_2,
):
    nc = tc.nc
    with ExitStack() as ctx:
        ctx.enter_context(tc.manual_schedule())
        keep = ctx.enter_context(tc.tile_pool(name="keep", bufs=1))
        work = ctx.enter_context(tc.tile_pool(name="work", bufs=3 * TOKEN_TILES * BANKS))
        psum = ctx.enter_context(tc.psum_pool(name="psum", bufs=8))

        identity = keep.tile([P, P], F32, name="identity")
        make_identity(nc, identity[:])
        ones = keep.tile([P, P], BF16, name="ones")
        nc.vector.memset(ones[:], 1.0)
        weight_q = weight_tiles(nc, keep, "q")
        gain_rows = [keep.tile([P, HEAD_DIM], BF16, name="gain_row%d" % w) for w in range(2)]
        for w in range(2):
            nc.gpsimd.memset(gain_rows[w][:], 0.0)
        nc.gpsimd.dma_start(out=gain_rows[0][0:1, :], in_=norm_q_w.unsqueeze(0))
        idle = psum.tile([P, P], F32, name="idle", tag="bank")
        for i in range(WARM_UP):
            nc.tensor.matmul(out=idle[:], lhsT=ones[:], rhs=ones[:], start=True, stop=True)
        one = keep.tile([P, 1], F32, name="one")
        nc.vector.memset(one[:], 1.0)
        warm = keep.tile([P, 1], F32, name="warm")
        nc.scalar.activation(out=warm[:], in_=one[:], func=ACT.Abs_reciprocal_sqrt)
        x_rows = hidden_states.rearrange("b (m p) d -> m p (b d)", p=P)
        x_tiles = [keep.tile([P, D_MODEL], BF16, name="x_sb%d" % m) for m in range(TOKEN_TILES)]
        for g in range(PASSES):
            cols = slice(K_PASS * g, K_PASS * (g + 1))
            nc.sync.dma_start(out=x_tiles[0][:, cols], in_=x_rows[0][:, cols])
        nc.sync.dma_start(out=x_tiles[1][:], in_=x_rows[1])
        load_scales(nc, weight_q, w_q_scales)
        load_words(nc, weight_q, w_q_words, 0)
        rotation = keep.tile([P, TOKEN_TILES, 2, 2, PAIRS], BF16, name="rotation")
        nc.sync.dma_start(out=rotation[:, :, 0, 0, :], in_=cos.rearrange("(m p) i -> p m i", p=P))
        nc.sync.dma_start(out=rotation[:, :, 0, 1, :], in_=sin.rearrange("(m p) i -> p m i", p=P))
        load_words(nc, weight_q, w_q_words, 1)
        nc.sync.dma_start(out=gain_rows[1][0:1, :], in_=norm_k_w.unsqueeze(0))
        weight_k = weight_tiles(nc, keep, "k")
        weight_v = weight_tiles(nc, keep, "v")
        load_words(nc, weight_k, w_k_words, 0)
        load_scales(nc, weight_k, w_k_scales)
        load_words(nc, weight_k, w_k_words, 1)
        load_words(nc, weight_v, w_v_words, 0)
        load_words(nc, weight_v, w_v_words, 1)
        load_scales(nc, weight_v, w_v_scales)

        x_mx = [quantise_tokens(nc, keep, psum, m, x_tiles[m], identity) for m in range(TOKEN_TILES)]
        nc.vector.tensor_scalar_mul(out=rotation[:, :, 1, 0, :], in0=rotation[:, :, 0, 1, :], scalar1=-1.0)
        nc.vector.tensor_copy(out=rotation[:, :, 1, 1, :], in_=rotation[:, :, 0, 0, :])
        outs = [o.rearrange("b (m p) h d -> m p (b h) d", p=P) for o in (out_0, out_1, out_2)]
        heads = [slice(BANK_HEADS * bank, BANK_HEADS * (bank + 1)) for bank in range(BANKS)]

        order = [(m, w, bank) for m in range(TOKEN_TILES) for w in range(2) for bank in range(BANKS)]
        last = len(order) - 1
        accs = []
        sums = []
        factors = []

        def finish(n):
            m, w, bank = order[n]
            adder = nc.vector if n == last else nc.gpsimd
            pieces = 2 if n == last else 1
            finished = norm_and_rotate(nc, work, adder, pieces, accs[n], factors[n], tables[(m, w)][:])
            if n < last:
                nc.sync.dma_start(out=outs[w][m][:, heads[bank], :], in_=finished[:])
            return finished

        copied = [work.tile([P, HEADS, HEAD_DIM], F32, name="values") for m in range(TOKEN_TILES)]

        def values(m, bank):
            acc_v = project(nc, psum, x_mx[m], weight_v[0], weight_v[1], bank)
            nc.scalar.copy(out=copied[m][:, heads[bank], :].rearrange("p h d -> p (h d)"), in_=acc_v[:])
            if bank == BANKS - 1:
                nc.scalar.dma_start(out=outs[2][m], in_=copied[m][:])

        for n, (m, w, bank) in enumerate(order):
            words, planes = (weight_q, weight_k)[w]
            if n == 0:
                accs.append(
                    project_pair(nc, psum, x_mx[m], words, planes, bank, 0)
                    + project_pair(nc, psum, x_mx[m], words, planes, bank, 1)
                )
                gain_q = spread_gain(nc, psum, ones, gain_rows[0])
                tables = {(0, 0): rotary_table(nc.vector, keep, 0, 0, rotation, gain_q)}
                gain_q_sb = keep.tile([P, HEAD_DIM], F32, name="gain_q_sb")
                nc.vector.tensor_copy(out=gain_q_sb[:], in_=gain_q[:])
                tables[(1, 0)] = rotary_table(nc.gpsimd, keep, 1, 0, rotation, gain_q_sb)
            else:
                accs.append(by_head(project(nc, psum, x_mx[m], words, planes, bank)))
            squares = work.tile([P, BANK_COLS], BF16, name="squares")
            sums.append(work.tile([P, BANK_HEADS], F32, name="sum_sq"))
            factors.append(work.tile([P, BANK_HEADS], F32, name="inv_rms"))
            sum_squares(nc, squares, sums[n], accs[n], 0, 2)
            if n == 0:
                inverse_rms(nc, factors[n], sums[n], 0, 2)
            elif n > DIRECT:
                inverse_rms(nc, factors[n - 1], sums[n - 1], 0, BANK_HEADS)
                finish(n - 1)
            sum_squares(nc, squares, sums[n], accs[n], 2, BANK_HEADS)
            if n < DIRECT:
                inverse_rms(nc, factors[n], sums[n], 2 if n == 0 else 0, BANK_HEADS)
            if n == 1:
                gain_k = spread_gain(nc, psum, ones, gain_rows[1])
                for tile in range(TOKEN_TILES):
                    tables[(tile, 1)] = rotary_table(nc.vector, keep, tile, 1, rotation, gain_k)
            if n < DIRECT:
                finish(n)
        inverse_rms(nc, factors[last], sums[last], 0, BANK_HEADS)
        values(0, 0)
        last_finished = finish(last)
        values(0, 1)
        values(1, 0)
        values(1, 1)
        nc.scalar.dma_start(out=outs[1][TOKEN_TILES - 1][:, heads[BANKS - 1], :], in_=last_finished[:])
